import numpy as np
import ml_dtypes


def mxq(x, axis, fmt="e4m3"):
    dtype, down = {"e4m3": (ml_dtypes.float8_e4m3fn, 7), "e5m2": (ml_dtypes.float8_e5m2, 14)}[fmt]
    v = np.moveaxis(np.asarray(x, np.float32).astype(ml_dtypes.bfloat16).astype(np.float64), axis, -1)
    blocks = v.reshape(v.shape[:-1] + (-1, 32))
    amax = np.abs(blocks).max(-1, keepdims=True)
    byte = np.maximum(np.where(amax > 0, np.frexp(amax)[1] - 1 + 127, 0) - down, 1)
    scale = np.exp2(byte - 127.0)
    codes = (blocks / scale).astype(np.float32).astype(dtype).astype(np.float64)
    return np.moveaxis((codes * scale).reshape(v.shape), -1, axis)


WIDE = False


def mx_kscale(k):
    if not WIDE:
        return np.ones(k)
    levels = np.array([10, -10, 5, -5, 0])
    a = np.random.permutation(np.resize(levels, k // 512 * 4)).reshape(k // 512, 4)
    idx = np.arange(k)
    return np.exp2(a[idx // 512, idx % 128 // 32])


BF16 = ml_dtypes.bfloat16


def bf(x):
    return np.asarray(x, np.float32).astype(BF16)


def f64(x):
    return np.asarray(x).astype(np.float64)


B, LQ, LK, D = 2, 512, 512, 512
EPS = 1e-8


def softmax(v):
    e = np.exp(v - v.max(-1, keepdims=True))
    return e / e.sum(-1, keepdims=True)


def setup_inputs():
    s = mx_kscale(D)
    g = np.sqrt(max(np.mean(s * s), np.mean(1.0 / (s * s))))
    base = np.array([0.0, 1.5, 0.5 - np.log(g)])
    return {
        "q_tanh": bf(np.tanh(np.random.standard_normal((B, LQ, D))) * s),
        "k_tanh": bf(np.tanh(np.random.standard_normal((B, LK, D))) / s),
        "value": bf(np.random.standard_normal((B, LK, D)) * 2.0),
        "scoring_weights": bf(base + 0.1 * np.random.standard_normal(base.shape)),
    }


def reference(q_tanh, k_tanh, value, scoring_weights):
    q, k = f64(q_tanh), f64(k_tanh)
    dot = mxq(q, 2, "e4m3") @ mxq(k, 2, "e4m3").transpose(0, 2, 1)
    qn = np.sqrt((q * q).sum(-1))
    kn = np.sqrt((k * k).sum(-1))
    cos = dot / np.maximum(qn[:, :, None] * kn[:, None, :], EPS)
    sq = np.maximum(qn[:, :, None] ** 2 + kn[:, None, :] ** 2 - 2.0 * dot, 0.0)
    euc = -np.sqrt(sq)
    w = softmax(f64(scoring_weights))
    scores = w[0] * dot + w[1] * cos + w[2] * euc
    attn = softmax(scores)
    return mxq(attn, 2, "e4m3") @ mxq(f64(value), 1, "e4m3")

@@ -1,0 +1,294 @@
+from contextlib import ExitStack
+
+import concourse.mybir as mybir
+from concourse.masks import make_identity
+
+F32 = mybir.dt.float32
+BF16 = mybir.dt.bfloat16
+U32 = mybir.dt.uint32
+U8 = mybir.dt.uint8
+FP8X4 = mybir.dt.float8_e4m3fn_x4
+ACT = mybir.ActivationFunctionType
+ALU = mybir.AluOpType
+AXIS = mybir.AxisListType
+
+B, LQ, LK, D = 2, 512, 512, 512
+P = 128
+PACK = 4
+HALVES = 2
+ROW_TILES = LQ // P
+N_TILES = B * ROW_TILES
+EPS = 1e-8
+TINY = 2.0**-116
+FLOPS = B * 2 * (2 * LQ * LK * D)
+
+
+def tile_adaptiveattention_pb_kernel(tc, q_tanh, k_tanh, value, scoring_weights, out):
+    nc = tc.nc
+    with ExitStack() as ctx:
+        keep = ctx.enter_context(tc.tile_pool(name="keep", bufs=1))
+        batch = ctx.enter_context(tc.tile_pool(name="batch", bufs=ROW_TILES))
+        work = ctx.enter_context(tc.tile_pool(name="work", bufs=3))
+        psum_t = ctx.enter_context(tc.psum_pool(name="psum_t", bufs=4))
+        psum_mx = ctx.enter_context(tc.psum_pool(name="psum_mx", bufs=4))
+        ctx.enter_context(tc.manual_schedule())
+
+        ident = keep.tile([P, P], F32)
+        k_sb = [keep.tile([P, ROW_TILES, D], BF16, name="k_sb%d" % b) for b in range(B)]
+        q_sb = [keep.tile([P, ROW_TILES, D], BF16, name="q_sb%d" % b) for b in range(B)]
+        v_sb = [keep.tile([P, PACK, D], BF16, name="v_sb%d" % b) for b in range(B)]
+        k_grouped = [keep.tile([P, LK, PACK], BF16, name="k_grouped%d" % b, align_bytes=64) for b in range(B)]
+        q_grouped = [keep.tile([P, LQ, PACK], BF16, name="q_grouped%d" % b, align_bytes=64) for b in range(B)]
+        v_grouped = [keep.tile([P, D, PACK], BF16, name="v_grouped%d" % b, align_bytes=64) for b in range(B)]
+        k_codes = [keep.tile([P, LK], U32, name="k_codes%d" % b, align_bytes=64) for b in range(B)]
+        q_codes = [keep.tile([P, LQ], U32, name="q_codes%d" % b, align_bytes=64) for b in range(B)]
+        v_codes = [keep.tile([P, D], U32, name="v_codes%d" % b, align_bytes=64) for b in range(B)]
+        k_scales = [keep.tile([P, LK], U8, name="k_scales%d" % b, align_bytes=64) for b in range(B)]
+        q_scales = [keep.tile([P, LQ], U8, name="q_scales%d" % b, align_bytes=64) for b in range(B)]
+        v_scales = [keep.tile([P, D], U8, name="v_scales%d" % b, align_bytes=64) for b in range(B)]
+        kn2 = [keep.tile([P, ROW_TILES], F32, name="kn2_%d" % b) for b in range(B)]
+        qn2 = [keep.tile([P, ROW_TILES], F32, name="qn2_%d" % b) for b in range(B)]
+        kn = [keep.tile([P, ROW_TILES], F32, name="kn_%d" % b) for b in range(B)]
+        qn = [keep.tile([P, ROW_TILES], F32, name="qn_%d" % b) for b in range(B)]
+        inv_kn = [keep.tile([P, ROW_TILES], F32, name="inv_kn%d" % b) for b in range(B)]
+        inv_qn = [keep.tile([P, ROW_TILES], F32, name="inv_qn%d" % b) for b in range(B)]
+        w1_inv_qn = [keep.tile([P, ROW_TILES], F32, name="w1_inv_qn%d" % b) for b in range(B)]
+        k_squares = [keep.tile([P, ROW_TILES, D], BF16, name="k_squares%d" % b) for b in range(B)]
+        q_squares = [keep.tile([P, ROW_TILES, D], BF16, name="q_squares%d" % b) for b in range(B)]
+        kn2_row = [keep.tile([P, LK], F32, name="kn2_row%d" % b) for b in range(B)]
+        inv_kn_row = [keep.tile([P, LK], F32, name="inv_kn_row%d" % b) for b in range(B)]
+        dot_cos = [keep.tile([P, LK], F32, name="dot_cos%d" % t) for t in range(N_TILES)]
+        dist = [keep.tile([P, LK], F32, name="dist%d" % t) for t in range(N_TILES)]
+        neg_max = keep.tile([P, N_TILES], F32)
+        exp_sum = keep.tile([P, N_TILES], F32)
+        inv_sum = keep.tile([P, N_TILES], F32)
+        tiny = keep.tile([P, 1], F32)
+
+        make_identity(nc, ident[:])
+        nc.vector.memset(tiny[:], TINY)
+
+        w_raw = keep.tile([P, 3], BF16)
+        nc.scalar.dma_start(out=w_raw[:], in_=scoring_weights.partition_broadcast(P))
+        for b in range(B):
+            nc.sync.dma_start(out=k_sb[b][:], in_=k_tanh[b].rearrange("(r p) d -> p r d", p=P))
+            nc.sync.dma_start(out=q_sb[b][:], in_=q_tanh[b].rearrange("(p r) d -> p r d", r=ROW_TILES))
+        for b in range(B):
+            nc.sync.dma_start(
+                out=v_sb[b][:].rearrange("p (u e) d -> p u (e d)", u=HALVES),
+                in_=value[b].rearrange("(u p e) d -> p u (e d)", u=HALVES, p=P),
+            )
+
+        w_neg_max = keep.tile([P, 1], F32)
+        w_exp = keep.tile([P, 3], F32)
+        w_sum = keep.tile([P, 1], F32)
+        w_inv_sum = keep.tile([P, 1], F32)
+        w = keep.tile([P, 3], F32)
+        cos_cap = keep.tile([P, 1], F32)
+        neg_w2 = keep.tile([P, 1], F32)
+        table_warm = keep.tile([P, 1], F32)
+        nc.vector.tensor_reduce(out=w_neg_max[:], in_=w_raw[:], axis=AXIS.X, op=ALU.max, negate=True)
+        nc.scalar.activation(out=w_exp[:], in_=w_raw[:], func=ACT.Exp, bias=w_neg_max[:], accum_out=w_sum[:])
+        nc.scalar.activation(out=table_warm[:], in_=w_sum[:], func=ACT.Sqrt)
+        nc.vector.reciprocal(out=w_inv_sum[:], in_=w_sum[:])
+        nc.vector.tensor_scalar(out=w[:], in0=w_exp[:], scalar1=w_inv_sum[:], scalar2=None, op0=ALU.mult)
+        nc.vector.tensor_scalar(out=cos_cap[:], in0=w[:, 1:2], scalar1=1.0 / EPS, scalar2=None, op0=ALU.mult)
+        nc.vector.tensor_scalar(out=neg_w2[:], in0=w[:, 2:3], scalar1=-1.0, scalar2=None, op0=ALU.mult)
+
+        def transpose_features(x_sb):
+            x_words = x_sb[:].bitcast(F32)
+            banks = {}
+            for pair in range(ROW_TILES // 2):
+                xt = psum_t.tile([P, HALVES, 2 * P], F32, tag="t", name="xt")
+                for i in range(2):
+                    for u in range(HALVES):
+                        nc.tensor.transpose(
+                            xt[:, u, i * P : (i + 1) * P],
+                            x_words[:, 2 * pair + i, u * P : (u + 1) * P],
+                            ident[:],
+                        )
+                banks[pair] = xt
+            return banks
+
+        def group_features(banks, x_grouped, copy):
+            grouped_words = x_grouped[:].bitcast(F32)
+            for pair in range(ROW_TILES // 2):
+                copy(
+                    out=grouped_words[:, 2 * pair * P : 2 * (pair + 1) * P, :],
+                    in_=banks[pair][:].rearrange("p u c -> p c u"),
+                )
+
+        def norms(x_sb, x_squares, xn2, xn):
+            for r in range(ROW_TILES):
+                nc.scalar.activation(
+                    out=x_squares[:, r, :], in_=x_sb[:, r, :], func=ACT.Square, accum_out=xn2[:, r : r + 1]
+                )
+            nc.scalar.activation(out=xn[:], in_=xn2[:], func=ACT.Sqrt, bias=tiny[:])
+
+        def quantise(x_grouped, x_codes, x_scales):
+            nc.vector.quantize_mx(
+                out=x_codes[:].bitcast(FP8X4),
+                scales=x_scales[:],
+                in_=x_grouped[:].rearrange("p c t -> p (c t)"),
+            )
+
+        def column_to_row(column):
+            row = psum_t.tile([P, LK], F32, tag="t", name="row")
+            for r in range(ROW_TILES):
+                nc.tensor.transpose(
+                    row[:, r * P : (r + 1) * P], column[:, r : r + 1].to_broadcast([P, P]), ident[:]
+                )
+            return row
+
+        def quantise_inputs_and_spread_key_norms(b):
+            quantise(k_grouped[b], k_codes[b], k_scales[b])
+            kn2_psum = column_to_row(kn2[b])
+            nc.vector.reciprocal(out=inv_kn[b][:], in_=kn[b][:])
+            inv_kn_psum = column_to_row(inv_kn[b])
+            quantise(q_grouped[b], q_codes[b], q_scales[b])
+            nc.vector.tensor_copy(out=kn2_row[b][:], in_=kn2_psum[:])
+            nc.vector.tensor_copy(out=inv_kn_row[b][:], in_=inv_kn_psum[:])
+
+        dot = {}
+
+        def squared_distances(b):
+            partial = {}
+            for r in range(ROW_TILES):
+                t = b * ROW_TILES + r
+                dot[t] = psum_mx.tile([P, LK], F32, tag="mx", name="dot")
+                nc.tensor.matmul_mx(
+                    out=dot[t][:],
+                    lhsT=q_codes[b][:, r * P : (r + 1) * P].bitcast(FP8X4),
+                    lhsT_scale=q_scales[b][:, r * P : (r + 1) * P],
+                    rhs=k_codes[b][:].bitcast(FP8X4),
+                    rhs_scale=k_scales[b][:],
+                    start=True,
+                    stop=True,
+                )
+                partial[r] = batch.tile([P, LK], F32, name="partial")
+                nc.vector.scalar_tensor_tensor(
+                    out=partial[r][:], in0=dot[t][:], scalar=-2.0, in1=kn2_row[b][:], op0=ALU.mult, op1=ALU.add
+                )
+            for r in range(ROW_TILES):
+                nc.vector.tensor_scalar(
+                    out=dist[b * ROW_TILES + r][:], in0=partial[r][:], scalar1=qn2[b][:, r : r + 1], scalar2=TINY,
+                    op0=ALU.add, op1=ALU.max,
+                )
+
+        def square_root(t):
+            nc.scalar.activation(out=dist[t][:], in_=dist[t][:], func=ACT.Sqrt)
+
+        def query_factors(b):
+            nc.vector.reciprocal(out=inv_qn[b][:], in_=qn[b][:])
+            nc.vector.tensor_scalar(out=w1_inv_qn[b][:], in0=inv_qn[b][:], scalar1=w[:, 1:2], scalar2=None, op0=ALU.mult)
+
+        def dot_and_cosine(t):
+            b, r = divmod(t, ROW_TILES)
+            cos_factor = work.tile([P, LK], F32)
+            nc.vector.tensor_scalar(
+                out=cos_factor[:], in0=inv_kn_row[b][:], scalar1=w1_inv_qn[b][:, r : r + 1], scalar2=cos_cap[:],
+                op0=ALU.mult, op1=ALU.min,
+            )
+            nc.vector.scalar_tensor_tensor(
+                out=dot_cos[t][:], in0=cos_factor[:], scalar=w[:, 0:1], in1=dot[t][:], op0=ALU.add, op1=ALU.mult
+            )
+
+        def prepare_values(b):
+            nc.vector.tensor_copy(out=v_grouped[b][:], in_=v_sb[b][:].rearrange("p t d -> p d t"))
+            quantise(v_grouped[b], v_codes[b], v_scales[b])
+
+        scores = {}
+        prob = {}
+        attn_t = {}
+        a_grouped = {}
+        product = {}
+
+        def final_scores(t):
+            scores[t] = work.tile([P, LK], F32, name="scores")
+            nc.vector.scalar_tensor_tensor(
+                out=scores[t][:], in0=dist[t][:], scalar=neg_w2[:], in1=dot_cos[t][:], op0=ALU.mult, op1=ALU.add
+            )
+            nc.vector.tensor_reduce(
+                out=neg_max[:, t : t + 1], in_=scores[t][:], axis=AXIS.X, op=ALU.max, negate=True
+            )
+
+        def exponentials(t):
+            prob[t] = work.tile([P, LK], F32, name="prob")
+            nc.scalar.activation(
+                out=prob[t][:], in_=scores[t][:], func=ACT.Exp, bias=neg_max[:, t : t + 1],
+                accum_out=exp_sum[:, t : t + 1],
+            )
+
+        def normalise_and_transpose(t):
+            nc.vector.reciprocal(out=inv_sum[:, t : t + 1], in_=exp_sum[:, t : t + 1])
+            attn = work.tile([P, LK], BF16)
+            nc.vector.tensor_scalar(
+                out=attn[:], in0=prob[t][:], scalar1=inv_sum[:, t : t + 1], scalar2=None, op0=ALU.mult
+            )
+            attn_words = attn[:].bitcast(F32)
+            attn_t[t] = psum_t.tile([P, HALVES, P], F32, tag="t", name="attn_t")
+            for u in range(HALVES):
+                nc.tensor.transpose(attn_t[t][:, u, :], attn_words[:, u * P : (u + 1) * P], ident[:])
+
+        def group_attention(t):
+            a_grouped[t] = work.tile([P, P, PACK], BF16, name="a_grouped", align_bytes=64)
+            nc.scalar.copy(out=a_grouped[t][:].bitcast(F32), in_=attn_t[t][:].rearrange("p u i -> p i u"))
+
+        def quantise_and_multiply(t):
+            b = t // ROW_TILES
+            a_codes = work.tile([P, P], U32, align_bytes=64)
+            a_scales = work.tile([P, P], U8, align_bytes=64)
+            quantise(a_grouped[t], a_codes, a_scales)
+            product[t] = psum_mx.tile([P, D], F32, tag="mx", name="product")
+            nc.tensor.matmul_mx(
+                out=product[t][:],
+                lhsT=a_codes[:].bitcast(FP8X4),
+                lhsT_scale=a_scales[:],
+                rhs=v_codes[b][:].bitcast(FP8X4),
+                rhs_scale=v_scales[b][:],
+                start=True,
+                stop=True,
+            )
+
+        def store(t):
+            b, r = divmod(t, ROW_TILES)
+            result = work.tile([P, D], F32)
+            nc.scalar.copy(out=result[:], in_=product[t][:])
+            nc.sync.dma_start(out=out[b].rearrange("(p r) d -> p r d", r=ROW_TILES)[:, r, :], in_=result[:])
+
+        group_features(transpose_features(k_sb[0]), k_grouped[0], nc.vector.tensor_copy)
+        group_features(transpose_features(q_sb[0]), q_grouped[0], nc.vector.tensor_copy)
+        k1_banks = transpose_features(k_sb[1])
+        norms(k_sb[0], k_squares[0], kn2[0], kn[0])
+        quantise_inputs_and_spread_key_norms(0)
+        norms(q_sb[0], q_squares[0], qn2[0], qn[0])
+        squared_distances(0)
+        group_features(k1_banks, k_grouped[1], nc.scalar.copy)
+        q1_banks = transpose_features(q_sb[1])
+        norms(k_sb[1], k_squares[1], kn2[1], kn[1])
+        group_features(q1_banks, q_grouped[1], nc.scalar.copy)
+        norms(q_sb[1], q_squares[1], qn2[1], qn[1])
+        query_factors(0)
+        for t in range(ROW_TILES):
+            dot_and_cosine(t)
+            square_root(t)
+        quantise_inputs_and_spread_key_norms(1)
+        squared_distances(1)
+        for t in range(ROW_TILES, N_TILES):
+            square_root(t)
+        query_factors(1)
+        for step in range(N_TILES + 4):
+            if 0 <= step - 1 < N_TILES:
+                exponentials(step - 1)
+            if 0 <= step - 4 < N_TILES:
+                store(step - 4)
+            if 0 <= step - 2 < N_TILES:
+                normalise_and_transpose(step - 2)
+                group_attention(step - 2)
+            if 0 <= step - 3 < N_TILES:
+                quantise_and_multiply(step - 3)
+            if step < N_TILES:
+                final_scores(step)
+            if step < B:
+                prepare_values(step)
+            if step < ROW_TILES:
+                dot_and_cosine(ROW_TILES + step)

@@ -91,7 +91,9 @@ def tile_adaptiveattention_pb_kernel(tc, q_tanh, k_tanh, value, scoring_weights,
         nc.scalar.activation(out=table_warm[:], in_=w_sum[:], func=ACT.Sqrt)
         nc.vector.reciprocal(out=w_inv_sum[:], in_=w_sum[:])
         nc.vector.tensor_scalar(out=w[:], in0=w_exp[:], scalar1=w_inv_sum[:], scalar2=None, op0=ALU.mult)
-        nc.vector.tensor_scalar(out=cos_cap[:], in0=w[:, 1:2], scalar1=1.0 / EPS, scalar2=None, op0=ALU.mult)
+        nc.vector.tensor_scalar(
+            out=cos_cap[:], in0=w[:, 1:2], scalar1=1.0 / EPS, scalar2=w[:, 0:1], op0=ALU.mult, op1=ALU.add
+        )
         nc.vector.tensor_scalar(out=neg_w2[:], in0=w[:, 2:3], scalar1=-1.0, scalar2=None, op0=ALU.mult)
 
         def transpose_features(x_sb):
@@ -139,19 +141,20 @@ def tile_adaptiveattention_pb_kernel(tc, q_tanh, k_tanh, value, scoring_weights,
                 )
             return row
 
-        def quantise_inputs_and_spread_key_norms(b):
+        def quantise_inputs_and_spread_key_norms(b, copy):
             quantise(k_grouped[b], k_codes[b], k_scales[b])
             kn2_psum = column_to_row(kn2[b])
             nc.vector.reciprocal(out=inv_kn[b][:], in_=kn[b][:])
             inv_kn_psum = column_to_row(inv_kn[b])
             quantise(q_grouped[b], q_codes[b], q_scales[b])
-            nc.vector.tensor_copy(out=kn2_row[b][:], in_=kn2_psum[:])
-            nc.vector.tensor_copy(out=inv_kn_row[b][:], in_=inv_kn_psum[:])
+            copy(out=kn2_row[b][:], in_=kn2_psum[:])
+            copy(out=inv_kn_row[b][:], in_=inv_kn_psum[:])
 
         dot = {}
+        partial = {}
+        cos_factor = {}
 
-        def squared_distances(b):
-            partial = {}
+        def dots(b):
             for r in range(ROW_TILES):
                 t = b * ROW_TILES + r
                 dot[t] = psum_mx.tile([P, LK], F32, tag="mx", name="dot")
@@ -164,15 +167,16 @@ def tile_adaptiveattention_pb_kernel(tc, q_tanh, k_tanh, value, scoring_weights,
                     start=True,
                     stop=True,
                 )
-                partial[r] = batch.tile([P, LK], F32, name="partial")
+                partial[t] = batch.tile([P, LK], F32, name="partial")
                 nc.vector.scalar_tensor_tensor(
-                    out=partial[r][:], in0=dot[t][:], scalar=-2.0, in1=kn2_row[b][:], op0=ALU.mult, op1=ALU.add
+                    out=partial[t][:], in0=dot[t][:], scalar=-2.0, in1=kn2_row[b][:], op0=ALU.mult, op1=ALU.add
                 )
-            for r in range(ROW_TILES):
-                nc.vector.tensor_scalar(
-                    out=dist[b * ROW_TILES + r][:], in0=partial[r][:], scalar1=qn2[b][:, r : r + 1], scalar2=TINY,
-                    op0=ALU.add, op1=ALU.max,
-                )
+
+        def squared_distance(t):
+            b, r = divmod(t, ROW_TILES)
+            nc.vector.tensor_scalar(
+                out=dist[t][:], in0=partial[t][:], scalar1=qn2[b][:, r : r + 1], scalar2=TINY, op0=ALU.add, op1=ALU.max
+            )
 
         def square_root(t):
             nc.scalar.activation(out=dist[t][:], in_=dist[t][:], func=ACT.Sqrt)
@@ -181,20 +185,24 @@ def tile_adaptiveattention_pb_kernel(tc, q_tanh, k_tanh, value, scoring_weights,
             nc.vector.reciprocal(out=inv_qn[b][:], in_=qn[b][:])
             nc.vector.tensor_scalar(out=w1_inv_qn[b][:], in0=inv_qn[b][:], scalar1=w[:, 1:2], scalar2=None, op0=ALU.mult)
 
-        def dot_and_cosine(t):
+        def cosine_factor(t):
             b, r = divmod(t, ROW_TILES)
-            cos_factor = work.tile([P, LK], F32)
-            nc.vector.tensor_scalar(
-                out=cos_factor[:], in0=inv_kn_row[b][:], scalar1=w1_inv_qn[b][:, r : r + 1], scalar2=cos_cap[:],
-                op0=ALU.mult, op1=ALU.min,
-            )
-            nc.vector.scalar_tensor_tensor(
-                out=dot_cos[t][:], in0=cos_factor[:], scalar=w[:, 0:1], in1=dot[t][:], op0=ALU.add, op1=ALU.mult
+            cos_factor[t] = batch.tile([P, LK], F32, name="cos_factor")
+            nc.gpsimd.tensor_scalar(
+                out=cos_factor[t][:], in0=inv_kn_row[b][:], scalar1=w1_inv_qn[b][:, r : r + 1], scalar2=w[:, 0:1],
+                op0=ALU.mult, op1=ALU.add,
             )
 
-        def prepare_values(b):
-            nc.vector.tensor_copy(out=v_grouped[b][:], in_=v_sb[b][:].rearrange("p t d -> p d t"))
-            quantise(v_grouped[b], v_codes[b], v_scales[b])
+        def dot_and_cosine(t):
+            nc.vector.scalar_tensor_tensor(
+                out=dot_cos[t][:], in0=cos_factor[t][:], scalar=cos_cap[:], in1=dot[t][:], op0=ALU.min, op1=ALU.mult
+            )
+
+        def regroup_values(b):
+            nc.gpsimd.tensor_scalar(
+                out=v_grouped[b][:], in0=v_sb[b][:].rearrange("p t d -> p d t"), scalar1=1.0, scalar2=0.0,
+                op0=ALU.mult, op1=ALU.add,
+            )
 
         scores = {}
         prob = {}
@@ -255,27 +263,34 @@ def tile_adaptiveattention_pb_kernel(tc, q_tanh, k_tanh, value, scoring_weights,
             nc.scalar.copy(out=result[:], in_=product[t][:])
             nc.sync.dma_start(out=out[b].rearrange("(p r) d -> p r d", r=ROW_TILES)[:, r, :], in_=result[:])
 
+        regroup_values(0)
         group_features(transpose_features(k_sb[0]), k_grouped[0], nc.vector.tensor_copy)
         group_features(transpose_features(q_sb[0]), q_grouped[0], nc.vector.tensor_copy)
         k1_banks = transpose_features(k_sb[1])
         norms(k_sb[0], k_squares[0], kn2[0], kn[0])
-        quantise_inputs_and_spread_key_norms(0)
+        quantise_inputs_and_spread_key_norms(0, nc.vector.tensor_copy)
         norms(q_sb[0], q_squares[0], qn2[0], qn[0])
-        squared_distances(0)
+        dots(0)
+        query_factors(0)
+        for t in range(ROW_TILES):
+            cosine_factor(t)
+            squared_distance(t)
+        regroup_values(1)
         group_features(k1_banks, k_grouped[1], nc.scalar.copy)
         q1_banks = transpose_features(q_sb[1])
         norms(k_sb[1], k_squares[1], kn2[1], kn[1])
         group_features(q1_banks, q_grouped[1], nc.scalar.copy)
         norms(q_sb[1], q_squares[1], qn2[1], qn[1])
-        query_factors(0)
         for t in range(ROW_TILES):
             dot_and_cosine(t)
             square_root(t)
-        quantise_inputs_and_spread_key_norms(1)
-        squared_distances(1)
-        for t in range(ROW_TILES, N_TILES):
-            square_root(t)
+        quantise_inputs_and_spread_key_norms(1, nc.scalar.copy)
+        dots(1)
         query_factors(1)
+        for t in range(ROW_TILES, N_TILES):
+            cosine_factor(t)
+            squared_distance(t)
+            square_root(t)
         for step in range(N_TILES + 4):
             if 0 <= step - 1 < N_TILES:
                 exponentials(step - 1)
@@ -289,6 +304,6 @@ def tile_adaptiveattention_pb_kernel(tc, q_tanh, k_tanh, value, scoring_weights,
             if step < N_TILES:
                 final_scores(step)
             if step < B:
-                prepare_values(step)
+                quantise(v_grouped[step], v_codes[step], v_scales[step])
             if step < ROW_TILES:
                 dot_and_cosine(ROW_TILES + step)

@@ -28,7 +28,7 @@ def tile_adaptiveattention_pb_kernel(tc, q_tanh, k_tanh, value, scoring_weights,
     with ExitStack() as ctx:
         keep = ctx.enter_context(tc.tile_pool(name="keep", bufs=1))
         batch = ctx.enter_context(tc.tile_pool(name="batch", bufs=ROW_TILES))
-        work = ctx.enter_context(tc.tile_pool(name="work", bufs=3))
+        work = ctx.enter_context(tc.tile_pool(name="work", bufs=4))
         psum_t = ctx.enter_context(tc.psum_pool(name="psum_t", bufs=4))
         psum_mx = ctx.enter_context(tc.psum_pool(name="psum_mx", bufs=4))
         ctx.enter_context(tc.manual_schedule())
@@ -52,11 +52,10 @@ def tile_adaptiveattention_pb_kernel(tc, q_tanh, k_tanh, value, scoring_weights,
         qn = [keep.tile([P, ROW_TILES], F32, name="qn_%d" % b) for b in range(B)]
         inv_kn = [keep.tile([P, ROW_TILES], F32, name="inv_kn%d" % b) for b in range(B)]
         inv_qn = [keep.tile([P, ROW_TILES], F32, name="inv_qn%d" % b) for b in range(B)]
-        w1_inv_qn = [keep.tile([P, ROW_TILES], F32, name="w1_inv_qn%d" % b) for b in range(B)]
         k_squares = [keep.tile([P, ROW_TILES, D], BF16, name="k_squares%d" % b) for b in range(B)]
         q_squares = [keep.tile([P, ROW_TILES, D], BF16, name="q_squares%d" % b) for b in range(B)]
         kn2_row = [keep.tile([P, LK], F32, name="kn2_row%d" % b) for b in range(B)]
-        inv_kn_row = [keep.tile([P, LK], F32, name="inv_kn_row%d" % b) for b in range(B)]
+        w1_inv_kn_row = [keep.tile([P, LK], F32, name="w1_inv_kn_row%d" % b) for b in range(B)]
         dot_cos = [keep.tile([P, LK], F32, name="dot_cos%d" % t) for t in range(N_TILES)]
         dist = [keep.tile([P, LK], F32, name="dist%d" % t) for t in range(N_TILES)]
         neg_max = keep.tile([P, N_TILES], F32)
@@ -70,9 +69,14 @@ def tile_adaptiveattention_pb_kernel(tc, q_tanh, k_tanh, value, scoring_weights,
         w_raw = keep.tile([P, 3], BF16)
         nc.scalar.dma_start(out=w_raw[:], in_=scoring_weights.partition_broadcast(P))
         for b in range(B):
-            nc.sync.dma_start(out=k_sb[b][:], in_=k_tanh[b].rearrange("(r p) d -> p r d", p=P))
+            k_rows = k_tanh[b].rearrange("(r p) d -> p r d", p=P)
+            pieces = 2 if b == 0 else 1
+            tiles = ROW_TILES // pieces
+            for i in range(pieces):
+                nc.sync.dma_start(
+                    out=k_sb[b][:, i * tiles : (i + 1) * tiles, :], in_=k_rows[:, i * tiles : (i + 1) * tiles, :]
+                )
             nc.sync.dma_start(out=q_sb[b][:], in_=q_tanh[b].rearrange("(p r) d -> p r d", r=ROW_TILES))
-        for b in range(B):
             nc.sync.dma_start(
                 out=v_sb[b][:].rearrange("p (u e) d -> p u (e d)", u=HALVES),
                 in_=value[b].rearrange("(u p e) d -> p u (e d)", u=HALVES, p=P),
@@ -85,16 +89,14 @@ def tile_adaptiveattention_pb_kernel(tc, q_tanh, k_tanh, value, scoring_weights,
         w = keep.tile([P, 3], F32)
         cos_cap = keep.tile([P, 1], F32)
         neg_w2 = keep.tile([P, 1], F32)
-        table_warm = keep.tile([P, 1], F32)
         nc.vector.tensor_reduce(out=w_neg_max[:], in_=w_raw[:], axis=AXIS.X, op=ALU.max, negate=True)
         nc.scalar.activation(out=w_exp[:], in_=w_raw[:], func=ACT.Exp, bias=w_neg_max[:], accum_out=w_sum[:])
-        nc.scalar.activation(out=table_warm[:], in_=w_sum[:], func=ACT.Sqrt)
         nc.vector.reciprocal(out=w_inv_sum[:], in_=w_sum[:])
-        nc.vector.tensor_scalar(out=w[:], in0=w_exp[:], scalar1=w_inv_sum[:], scalar2=None, op0=ALU.mult)
-        nc.vector.tensor_scalar(
+        nc.gpsimd.tensor_scalar(out=w[:], in0=w_exp[:], scalar1=w_inv_sum[:], scalar2=0.0, op0=ALU.mult, op1=ALU.add)
+        nc.gpsimd.tensor_scalar(
             out=cos_cap[:], in0=w[:, 1:2], scalar1=1.0 / EPS, scalar2=w[:, 0:1], op0=ALU.mult, op1=ALU.add
         )
-        nc.vector.tensor_scalar(out=neg_w2[:], in0=w[:, 2:3], scalar1=-1.0, scalar2=None, op0=ALU.mult)
+        nc.gpsimd.tensor_scalar(out=neg_w2[:], in0=w[:, 2:3], scalar1=-1.0, scalar2=0.0, op0=ALU.mult, op1=ALU.add)
 
         def transpose_features(x_sb):
             x_words = x_sb[:].bitcast(F32)
@@ -133,44 +135,34 @@ def tile_adaptiveattention_pb_kernel(tc, q_tanh, k_tanh, value, scoring_weights,
                 in_=x_grouped[:].rearrange("p c t -> p (c t)"),
             )
 
-        def column_to_row(column):
-            row = psum_t.tile([P, LK], F32, tag="t", name="row")
+        def spread(column, row_sb, copy):
+            row = psum_t.tile([P, LK], F32, tag="t")
             for r in range(ROW_TILES):
                 nc.tensor.transpose(
                     row[:, r * P : (r + 1) * P], column[:, r : r + 1].to_broadcast([P, P]), ident[:]
                 )
-            return row
-
-        def quantise_inputs_and_spread_key_norms(b, copy):
-            quantise(k_grouped[b], k_codes[b], k_scales[b])
-            kn2_psum = column_to_row(kn2[b])
-            nc.vector.reciprocal(out=inv_kn[b][:], in_=kn[b][:])
-            inv_kn_psum = column_to_row(inv_kn[b])
-            quantise(q_grouped[b], q_codes[b], q_scales[b])
-            copy(out=kn2_row[b][:], in_=kn2_psum[:])
-            copy(out=inv_kn_row[b][:], in_=inv_kn_psum[:])
+            copy(out=row_sb[:], in_=row[:])
 
         dot = {}
         partial = {}
         cos_factor = {}
 
-        def dots(b):
-            for r in range(ROW_TILES):
-                t = b * ROW_TILES + r
-                dot[t] = psum_mx.tile([P, LK], F32, tag="mx", name="dot")
-                nc.tensor.matmul_mx(
-                    out=dot[t][:],
-                    lhsT=q_codes[b][:, r * P : (r + 1) * P].bitcast(FP8X4),
-                    lhsT_scale=q_scales[b][:, r * P : (r + 1) * P],
-                    rhs=k_codes[b][:].bitcast(FP8X4),
-                    rhs_scale=k_scales[b][:],
-                    start=True,
-                    stop=True,
-                )
-                partial[t] = batch.tile([P, LK], F32, name="partial")
-                nc.vector.scalar_tensor_tensor(
-                    out=partial[t][:], in0=dot[t][:], scalar=-2.0, in1=kn2_row[b][:], op0=ALU.mult, op1=ALU.add
-                )
+        def dot_and_partial(t):
+            b, r = divmod(t, ROW_TILES)
+            dot[t] = psum_mx.tile([P, LK], F32, tag="mx", name="dot")
+            nc.tensor.matmul_mx(
+                out=dot[t][:],
+                lhsT=q_codes[b][:, r * P : (r + 1) * P].bitcast(FP8X4),
+                lhsT_scale=q_scales[b][:, r * P : (r + 1) * P],
+                rhs=k_codes[b][:].bitcast(FP8X4),
+                rhs_scale=k_scales[b][:],
+                start=True,
+                stop=True,
+            )
+            partial[t] = batch.tile([P, LK], F32, name="partial")
+            nc.vector.scalar_tensor_tensor(
+                out=partial[t][:], in0=dot[t][:], scalar=-2.0, in1=kn2_row[b][:], op0=ALU.mult, op1=ALU.add
+            )
 
         def squared_distance(t):
             b, r = divmod(t, ROW_TILES)
@@ -181,15 +173,12 @@ def tile_adaptiveattention_pb_kernel(tc, q_tanh, k_tanh, value, scoring_weights,
         def square_root(t):
             nc.scalar.activation(out=dist[t][:], in_=dist[t][:], func=ACT.Sqrt)
 
-        def query_factors(b):
-            nc.vector.reciprocal(out=inv_qn[b][:], in_=qn[b][:])
-            nc.vector.tensor_scalar(out=w1_inv_qn[b][:], in0=inv_qn[b][:], scalar1=w[:, 1:2], scalar2=None, op0=ALU.mult)
 
         def cosine_factor(t):
             b, r = divmod(t, ROW_TILES)
             cos_factor[t] = batch.tile([P, LK], F32, name="cos_factor")
             nc.gpsimd.tensor_scalar(
-                out=cos_factor[t][:], in0=inv_kn_row[b][:], scalar1=w1_inv_qn[b][:, r : r + 1], scalar2=w[:, 0:1],
+                out=cos_factor[t][:], in0=w1_inv_kn_row[b][:], scalar1=inv_qn[b][:, r : r + 1], scalar2=w[:, 0:1],
                 op0=ALU.mult, op1=ALU.add,
             )
 
@@ -199,10 +188,12 @@ def tile_adaptiveattention_pb_kernel(tc, q_tanh, k_tanh, value, scoring_weights,
             )
 
         def regroup_values(b):
-            nc.gpsimd.tensor_scalar(
-                out=v_grouped[b][:], in0=v_sb[b][:].rearrange("p t d -> p d t"), scalar1=1.0, scalar2=0.0,
-                op0=ALU.mult, op1=ALU.add,
-            )
+            for c in range(D // P):
+                cols = slice(c * P, (c + 1) * P)
+                nc.gpsimd.tensor_scalar(
+                    out=v_grouped[b][:, cols, :], in0=v_sb[b][:, :, cols].rearrange("p t d -> p d t"),
+                    scalar1=1.0, scalar2=0.0, op0=ALU.mult, op1=ALU.add,
+                )
 
         scores = {}
         prob = {}
@@ -229,9 +220,12 @@ def tile_adaptiveattention_pb_kernel(tc, q_tanh, k_tanh, value, scoring_weights,
         def normalise_and_transpose(t):
             nc.vector.reciprocal(out=inv_sum[:, t : t + 1], in_=exp_sum[:, t : t + 1])
             attn = work.tile([P, LK], BF16)
-            nc.vector.tensor_scalar(
-                out=attn[:], in0=prob[t][:], scalar1=inv_sum[:, t : t + 1], scalar2=None, op0=ALU.mult
-            )
+            if t >= ROW_TILES:
+                nc.vector.tensor_scalar(
+                    out=attn[:], in0=prob[t][:], scalar1=inv_sum[:, t : t + 1], scalar2=None, op0=ALU.mult
+                )
+            else:
+                nc.scalar.activation(out=attn[:], in_=prob[t][:], func=ACT.Copy, scale=inv_sum[:, t : t + 1])
             attn_words = attn[:].bitcast(F32)
             attn_t[t] = psum_t.tile([P, HALVES, P], F32, tag="t", name="attn_t")
             for u in range(HALVES):
@@ -263,44 +257,62 @@ def tile_adaptiveattention_pb_kernel(tc, q_tanh, k_tanh, value, scoring_weights,
             nc.scalar.copy(out=result[:], in_=product[t][:])
             nc.sync.dma_start(out=out[b].rearrange("(p r) d -> p r d", r=ROW_TILES)[:, r, :], in_=result[:])
 
+        def scaled_by_w1(out, in_):
+            nc.scalar.activation(out=out, in_=in_, func=ACT.Copy, scale=w[:, 1:2])
+
+        def products(b):
+            first = b * ROW_TILES
+            dot_and_partial(first)
+            nc.vector.reciprocal(out=inv_qn[b][:], in_=qn[b][:])
+            for t in range(first + 1, first + ROW_TILES):
+                dot_and_partial(t)
+            for t in range(first, first + ROW_TILES):
+                cosine_factor(t)
+
         regroup_values(0)
         group_features(transpose_features(k_sb[0]), k_grouped[0], nc.vector.tensor_copy)
         group_features(transpose_features(q_sb[0]), q_grouped[0], nc.vector.tensor_copy)
-        k1_banks = transpose_features(k_sb[1])
         norms(k_sb[0], k_squares[0], kn2[0], kn[0])
-        quantise_inputs_and_spread_key_norms(0, nc.vector.tensor_copy)
+        quantise(k_grouped[0], k_codes[0], k_scales[0])
+        quantise(q_grouped[0], q_codes[0], q_scales[0])
+        spread(kn2[0], kn2_row[0], nc.vector.tensor_copy)
+        nc.vector.reciprocal(out=inv_kn[0][:], in_=kn[0][:])
+        k1_banks = transpose_features(k_sb[1])
         norms(q_sb[0], q_squares[0], qn2[0], qn[0])
-        dots(0)
-        query_factors(0)
-        for t in range(ROW_TILES):
-            cosine_factor(t)
-            squared_distance(t)
+        spread(inv_kn[0], w1_inv_kn_row[0], scaled_by_w1)
+        products(0)
         regroup_values(1)
         group_features(k1_banks, k_grouped[1], nc.scalar.copy)
         q1_banks = transpose_features(q_sb[1])
         norms(k_sb[1], k_squares[1], kn2[1], kn[1])
         group_features(q1_banks, q_grouped[1], nc.scalar.copy)
+        spread(kn2[1], kn2_row[1], nc.scalar.copy)
         norms(q_sb[1], q_squares[1], qn2[1], qn[1])
         for t in range(ROW_TILES):
             dot_and_cosine(t)
+        nc.vector.reciprocal(out=inv_kn[1][:], in_=kn[1][:])
+        quantise(k_grouped[1], k_codes[1], k_scales[1])
+        quantise(q_grouped[1], q_codes[1], q_scales[1])
+        for t in range(ROW_TILES):
+            squared_distance(t)
+        spread(inv_kn[1], w1_inv_kn_row[1], scaled_by_w1)
+        for t in range(ROW_TILES):
             square_root(t)
-        quantise_inputs_and_spread_key_norms(1, nc.scalar.copy)
-        dots(1)
-        query_factors(1)
+        products(1)
         for t in range(ROW_TILES, N_TILES):
-            cosine_factor(t)
             squared_distance(t)
             square_root(t)
-        for step in range(N_TILES + 4):
+        for step in range(N_TILES + 5):
+            if 0 <= step - 3 < N_TILES:
+                group_attention(step - 3)
             if 0 <= step - 1 < N_TILES:
                 exponentials(step - 1)
-            if 0 <= step - 4 < N_TILES:
-                store(step - 4)
             if 0 <= step - 2 < N_TILES:
                 normalise_and_transpose(step - 2)
-                group_attention(step - 2)
-            if 0 <= step - 3 < N_TILES:
-                quantise_and_multiply(step - 3)
+            if 0 <= step - 5 < N_TILES:
+                store(step - 5)
+            if 0 <= step - 4 < N_TILES:
+                quantise_and_multiply(step - 4)
             if step < N_TILES:
                 final_scores(step)
             if step < B:

@@ -206,6 +206,8 @@ def tile_adaptiveattention_pb_kernel(tc, q_tanh, k_tanh, value, scoring_weights,
             nc.vector.scalar_tensor_tensor(
                 out=scores[t][:], in0=dist[t][:], scalar=neg_w2[:], in1=dot_cos[t][:], op0=ALU.mult, op1=ALU.add
             )
+
+        def row_maximum(t):
             nc.vector.tensor_reduce(
                 out=neg_max[:, t : t + 1], in_=scores[t][:], axis=AXIS.X, op=ALU.max, negate=True
             )
@@ -217,8 +219,10 @@ def tile_adaptiveattention_pb_kernel(tc, q_tanh, k_tanh, value, scoring_weights,
                 accum_out=exp_sum[:, t : t + 1],
             )
 
-        def normalise_and_transpose(t):
+        def reciprocal_of_sum(t):
             nc.vector.reciprocal(out=inv_sum[:, t : t + 1], in_=exp_sum[:, t : t + 1])
+
+        def normalise_and_transpose(t):
             attn = work.tile([P, LK], BF16)
             if t >= ROW_TILES:
                 nc.vector.tensor_scalar(
@@ -308,14 +312,18 @@ def tile_adaptiveattention_pb_kernel(tc, q_tanh, k_tanh, value, scoring_weights,
             if 0 <= step - 1 < N_TILES:
                 exponentials(step - 1)
             if 0 <= step - 2 < N_TILES:
+                reciprocal_of_sum(step - 2)
+            if step < N_TILES:
+                final_scores(step)
+            if 0 <= step - 2 < N_TILES:
                 normalise_and_transpose(step - 2)
             if 0 <= step - 5 < N_TILES:
                 store(step - 5)
             if 0 <= step - 4 < N_TILES:
                 quantise_and_multiply(step - 4)
-            if step < N_TILES:
-                final_scores(step)
-            if step < B:
-                quantise(v_grouped[step], v_codes[step], v_scales[step])
             if step < ROW_TILES:
                 dot_and_cosine(ROW_TILES + step)
+            if step < N_TILES:
+                row_maximum(step)
+            if step < B:
+                quantise(v_grouped[step], v_codes[step], v_scales[step])

@@ -18,6 +18,7 @@ PACK = 4
 HALVES = 2
 ROW_TILES = LQ // P
 N_TILES = B * ROW_TILES
+LAST_ON_VECTOR = 2
 EPS = 1e-8
 TINY = 2.0**-116
 FLOPS = B * 2 * (2 * LQ * LK * D)
@@ -224,12 +225,14 @@ def tile_adaptiveattention_pb_kernel(tc, q_tanh, k_tanh, value, scoring_weights,
 
         def normalise_and_transpose(t):
             attn = work.tile([P, LK], BF16)
-            if t >= ROW_TILES:
+            if t >= N_TILES - LAST_ON_VECTOR:
                 nc.vector.tensor_scalar(
                     out=attn[:], in0=prob[t][:], scalar1=inv_sum[:, t : t + 1], scalar2=None, op0=ALU.mult
                 )
             else:
-                nc.scalar.activation(out=attn[:], in_=prob[t][:], func=ACT.Copy, scale=inv_sum[:, t : t + 1])
+                nc.gpsimd.tensor_scalar(
+                    out=attn[:], in0=prob[t][:], scalar1=inv_sum[:, t : t + 1], scalar2=0.0, op0=ALU.mult, op1=ALU.add
+                )
             attn_words = attn[:].bitcast(F32)
             attn_t[t] = psum_t.tile([P, HALVES, P], F32, tag="t", name="attn_t")
             for u in range(HALVES):
@@ -261,14 +264,20 @@ def tile_adaptiveattention_pb_kernel(tc, q_tanh, k_tanh, value, scoring_weights,
             nc.scalar.copy(out=result[:], in_=product[t][:])
             nc.sync.dma_start(out=out[b].rearrange("(p r) d -> p r d", r=ROW_TILES)[:, r, :], in_=result[:])
 
-        def scaled_by_w1(out, in_):
+        def vector_scaled_by_w1(out, in_):
+            nc.vector.tensor_scalar(out=out, in0=in_, scalar1=w[:, 1:2], scalar2=None, op0=ALU.mult)
+
+        def scalar_scaled_by_w1(out, in_):
             nc.scalar.activation(out=out, in_=in_, func=ACT.Copy, scale=w[:, 1:2])
 
-        def products(b):
+        def products(b, scaled_by_w1):
             first = b * ROW_TILES
-            dot_and_partial(first)
+            half = first + ROW_TILES // 2
+            for t in range(first, half):
+                dot_and_partial(t)
+            spread(inv_kn[b], w1_inv_kn_row[b], scaled_by_w1)
             nc.vector.reciprocal(out=inv_qn[b][:], in_=qn[b][:])
-            for t in range(first + 1, first + ROW_TILES):
+            for t in range(half, first + ROW_TILES):
                 dot_and_partial(t)
             for t in range(first, first + ROW_TILES):
                 cosine_factor(t)
@@ -281,10 +290,9 @@ def tile_adaptiveattention_pb_kernel(tc, q_tanh, k_tanh, value, scoring_weights,
         quantise(q_grouped[0], q_codes[0], q_scales[0])
         spread(kn2[0], kn2_row[0], nc.vector.tensor_copy)
         nc.vector.reciprocal(out=inv_kn[0][:], in_=kn[0][:])
-        k1_banks = transpose_features(k_sb[1])
         norms(q_sb[0], q_squares[0], qn2[0], qn[0])
-        spread(inv_kn[0], w1_inv_kn_row[0], scaled_by_w1)
-        products(0)
+        k1_banks = transpose_features(k_sb[1])
+        products(0, vector_scaled_by_w1)
         regroup_values(1)
         group_features(k1_banks, k_grouped[1], nc.scalar.copy)
         q1_banks = transpose_features(q_sb[1])
@@ -299,10 +307,9 @@ def tile_adaptiveattention_pb_kernel(tc, q_tanh, k_tanh, value, scoring_weights,
         quantise(q_grouped[1], q_codes[1], q_scales[1])
         for t in range(ROW_TILES):
             squared_distance(t)
-        spread(inv_kn[1], w1_inv_kn_row[1], scaled_by_w1)
         for t in range(ROW_TILES):
             square_root(t)
-        products(1)
+        products(1, scalar_scaled_by_w1)
         for t in range(ROW_TILES, N_TILES):
             squared_distance(t)
             square_root(t)

@@ -1,3 +1,4 @@
+import math
 from contextlib import ExitStack
 
 import concourse.mybir as mybir
@@ -18,9 +19,11 @@ PACK = 4
 HALVES = 2
 ROW_TILES = LQ // P
 N_TILES = B * ROW_TILES
-LAST_ON_VECTOR = 2
+LOG2E = 1.0 / math.log(2.0)
 EPS = 1e-8
 TINY = 2.0**-116
+HUGE = 2.0**117
+ROOT_HALF = math.sqrt(0.5)
 FLOPS = B * 2 * (2 * LQ * LK * D)
 
 
@@ -30,11 +33,14 @@ def tile_adaptiveattention_pb_kernel(tc, q_tanh, k_tanh, value, scoring_weights,
         keep = ctx.enter_context(tc.tile_pool(name="keep", bufs=1))
         batch = ctx.enter_context(tc.tile_pool(name="batch", bufs=ROW_TILES))
         work = ctx.enter_context(tc.tile_pool(name="work", bufs=4))
+        scorep = ctx.enter_context(tc.tile_pool(name="scorep", bufs=6))
+        results = ctx.enter_context(tc.tile_pool(name="results", bufs=N_TILES))
         psum_t = ctx.enter_context(tc.psum_pool(name="psum_t", bufs=4))
         psum_mx = ctx.enter_context(tc.psum_pool(name="psum_mx", bufs=4))
         ctx.enter_context(tc.manual_schedule())
 
         ident = keep.tile([P, P], F32)
+        ones = keep.tile([P, P], BF16)
         k_sb = [keep.tile([P, ROW_TILES, D], BF16, name="k_sb%d" % b) for b in range(B)]
         q_sb = [keep.tile([P, ROW_TILES, D], BF16, name="q_sb%d" % b) for b in range(B)]
         v_sb = [keep.tile([P, PACK, D], BF16, name="v_sb%d" % b) for b in range(B)]
@@ -47,28 +53,32 @@ def tile_adaptiveattention_pb_kernel(tc, q_tanh, k_tanh, value, scoring_weights,
         k_scales = [keep.tile([P, LK], U8, name="k_scales%d" % b, align_bytes=64) for b in range(B)]
         q_scales = [keep.tile([P, LQ], U8, name="q_scales%d" % b, align_bytes=64) for b in range(B)]
         v_scales = [keep.tile([P, D], U8, name="v_scales%d" % b, align_bytes=64) for b in range(B)]
-        kn2 = [keep.tile([P, ROW_TILES], F32, name="kn2_%d" % b) for b in range(B)]
-        qn2 = [keep.tile([P, ROW_TILES], F32, name="qn2_%d" % b) for b in range(B)]
-        kn = [keep.tile([P, ROW_TILES], F32, name="kn_%d" % b) for b in range(B)]
-        qn = [keep.tile([P, ROW_TILES], F32, name="qn_%d" % b) for b in range(B)]
-        inv_kn = [keep.tile([P, ROW_TILES], F32, name="inv_kn%d" % b) for b in range(B)]
-        inv_qn = [keep.tile([P, ROW_TILES], F32, name="inv_qn%d" % b) for b in range(B)]
-        k_squares = [keep.tile([P, ROW_TILES, D], BF16, name="k_squares%d" % b) for b in range(B)]
-        q_squares = [keep.tile([P, ROW_TILES, D], BF16, name="q_squares%d" % b) for b in range(B)]
-        kn2_row = [keep.tile([P, LK], F32, name="kn2_row%d" % b) for b in range(B)]
-        w1_inv_kn_row = [keep.tile([P, LK], F32, name="w1_inv_kn_row%d" % b) for b in range(B)]
+        half_norm2 = [keep.tile([P, 2 * ROW_TILES], F32, name="half_norm2_%d" % b) for b in range(B)]
+        norm = [keep.tile([P, 2 * ROW_TILES], F32, name="norm_%d" % b) for b in range(B)]
+        inv_norm = [keep.tile([P, 2 * ROW_TILES], F32, name="inv_norm%d" % b) for b in range(B)]
+        w1_inv_qn = [keep.tile([P, ROW_TILES], F32, name="w1_inv_qn%d" % b) for b in range(B)]
+        half_kn2_row = [keep.tile([P, LK], F32, name="half_kn2_row%d" % b) for b in range(B)]
+        inv_kn_row = [keep.tile([P, LK], F32, name="inv_kn_row%d" % b) for b in range(B)]
         dot_cos = [keep.tile([P, LK], F32, name="dot_cos%d" % t) for t in range(N_TILES)]
         dist = [keep.tile([P, LK], F32, name="dist%d" % t) for t in range(N_TILES)]
         neg_max = keep.tile([P, N_TILES], F32)
         exp_sum = keep.tile([P, N_TILES], F32)
         inv_sum = keep.tile([P, N_TILES], F32)
         tiny = keep.tile([P, 1], F32)
+        tiny_root = keep.tile([P, 1], F32)
+        w_raw = keep.tile([P, PACK], BF16)
+        two = keep.tile([P, 3], F32)
+        minus_one = keep.tile([P, 1], F32)
 
-        make_identity(nc, ident[:])
+        nc.vector.memset(w_raw[:], 0.0)
         nc.vector.memset(tiny[:], TINY)
+        nc.scalar.dma_start(out=w_raw[0:1, 0:3], in_=scoring_weights.unsqueeze(0))
+        nc.scalar.activation(out=tiny_root[:], in_=tiny[:], func=ACT.Sqrt)
+        make_identity(nc, ident[:])
+        nc.gpsimd.memset(ones[:], 1.0)
+        nc.gpsimd.memset(two[:], 2.0)
+        nc.gpsimd.memset(minus_one[:], -1.0)
 
-        w_raw = keep.tile([P, 3], BF16)
-        nc.scalar.dma_start(out=w_raw[:], in_=scoring_weights.partition_broadcast(P))
         for b in range(B):
             k_rows = k_tanh[b].rearrange("(r p) d -> p r d", p=P)
             pieces = 2 if b == 0 else 1
@@ -77,27 +87,44 @@ def tile_adaptiveattention_pb_kernel(tc, q_tanh, k_tanh, value, scoring_weights,
                 nc.sync.dma_start(
                     out=k_sb[b][:, i * tiles : (i + 1) * tiles, :], in_=k_rows[:, i * tiles : (i + 1) * tiles, :]
                 )
-            nc.sync.dma_start(out=q_sb[b][:], in_=q_tanh[b].rearrange("(p r) d -> p r d", r=ROW_TILES))
+            q_rows = q_tanh[b].rearrange("(p r) d -> p r d", r=ROW_TILES)
+            for i in range(pieces):
+                nc.sync.dma_start(
+                    out=q_sb[b][:, i * tiles : (i + 1) * tiles, :], in_=q_rows[:, i * tiles : (i + 1) * tiles, :]
+                )
             nc.sync.dma_start(
                 out=v_sb[b][:].rearrange("p (u e) d -> p u (e d)", u=HALVES),
                 in_=value[b].rearrange("(u p e) d -> p u (e d)", u=HALVES, p=P),
             )
 
         w_neg_max = keep.tile([P, 1], F32)
+        w_log2 = keep.tile([P, 3], F32)
         w_exp = keep.tile([P, 3], F32)
         w_sum = keep.tile([P, 1], F32)
         w_inv_sum = keep.tile([P, 1], F32)
         w = keep.tile([P, 3], F32)
         cos_cap = keep.tile([P, 1], F32)
-        neg_w2 = keep.tile([P, 1], F32)
-        nc.vector.tensor_reduce(out=w_neg_max[:], in_=w_raw[:], axis=AXIS.X, op=ALU.max, negate=True)
-        nc.scalar.activation(out=w_exp[:], in_=w_raw[:], func=ACT.Exp, bias=w_neg_max[:], accum_out=w_sum[:])
-        nc.vector.reciprocal(out=w_inv_sum[:], in_=w_sum[:])
-        nc.gpsimd.tensor_scalar(out=w[:], in0=w_exp[:], scalar1=w_inv_sum[:], scalar2=0.0, op0=ALU.mult, op1=ALU.add)
-        nc.gpsimd.tensor_scalar(
-            out=cos_cap[:], in0=w[:, 1:2], scalar1=1.0 / EPS, scalar2=w[:, 0:1], op0=ALU.mult, op1=ALU.add
-        )
-        nc.gpsimd.tensor_scalar(out=neg_w2[:], in0=w[:, 2:3], scalar1=-1.0, scalar2=0.0, op0=ALU.mult, op1=ALU.add)
+        twice_w2_squared = keep.tile([P, 1], F32)
+
+        def mixing_weights():
+            w_all = psum_t.tile([P, 3], F32, tag="t", name="w_all")
+            nc.tensor.matmul(w_all[:], lhsT=ones[:], rhs=w_raw[:, 0:3], start=True, stop=True)
+            nc.vector.tensor_reduce(out=w_neg_max[:], in_=w_all[:], axis=AXIS.X, op=ALU.max, negate=True)
+            nc.vector.tensor_scalar(
+                out=w_log2[:], in0=w_all[:], scalar1=w_neg_max[:], scalar2=LOG2E, op0=ALU.add, op1=ALU.mult
+            )
+            nc.gpsimd.tensor_tensor(out=w_exp[:], in0=two[:], in1=w_log2[:], op=ALU.pow)
+            nc.gpsimd.tensor_scalar(
+                out=w_sum[:], in0=w_exp[:, 0:1], scalar1=w_exp[:, 1:2], scalar2=w_exp[:, 2:3], op0=ALU.add, op1=ALU.add
+            )
+            nc.gpsimd.tensor_tensor(out=w_inv_sum[:], in0=w_sum[:], in1=minus_one[:], op=ALU.pow)
+            nc.gpsimd.tensor_scalar(out=w[:], in0=w_exp[:], scalar1=w_inv_sum[:], scalar2=0.0, op0=ALU.mult, op1=ALU.add)
+            nc.gpsimd.tensor_scalar(
+                out=cos_cap[:], in0=w[:, 1:2], scalar1=1.0 / EPS, scalar2=w[:, 0:1], op0=ALU.mult, op1=ALU.add
+            )
+            nc.gpsimd.tensor_scalar(
+                out=twice_w2_squared[:], in0=w[:, 2:3], scalar1=w[:, 2:3], scalar2=2.0, op0=ALU.mult, op1=ALU.mult
+            )
 
         def transpose_features(x_sb):
             x_words = x_sb[:].bitcast(F32)
@@ -114,20 +141,44 @@ def tile_adaptiveattention_pb_kernel(tc, q_tanh, k_tanh, value, scoring_weights,
                 banks[pair] = xt
             return banks
 
-        def group_features(banks, x_grouped, copy):
+        def group_features(banks, pair, x_grouped, copy):
             grouped_words = x_grouped[:].bitcast(F32)
-            for pair in range(ROW_TILES // 2):
-                copy(
-                    out=grouped_words[:, 2 * pair * P : 2 * (pair + 1) * P, :],
-                    in_=banks[pair][:].rearrange("p u c -> p c u"),
-                )
+            copy(
+                out=grouped_words[:, 2 * pair * P : 2 * (pair + 1) * P, :],
+                in_=banks[pair][:].rearrange("p u c -> p c u"),
+            )
 
-        def norms(x_sb, x_squares, xn2, xn):
-            for r in range(ROW_TILES):
-                nc.scalar.activation(
-                    out=x_squares[:, r, :], in_=x_sb[:, r, :], func=ACT.Square, accum_out=xn2[:, r : r + 1]
+        def square(x_sb, b, first, r):
+            squares = work.tile([P, D], BF16, name="squares")
+            nc.scalar.activation(
+                out=squares[:], in_=x_sb[:, r, :], func=ACT.Square, scale=ROOT_HALF,
+                accum_out=half_norm2[b][:, first + r : first + r + 1],
+            )
+
+        def squares_on_tensor(x_grouped, b, first, r):
+            gram = psum_t.tile([P, P], F32, tag="t", name="gram")
+            rows = slice(r * P, (r + 1) * P)
+            for j in range(PACK):
+                nc.tensor.matmul(
+                    gram[:], lhsT=x_grouped[:, rows, j], rhs=x_grouped[:, rows, j], start=(j == 0), stop=(j == PACK - 1)
                 )
-            nc.scalar.activation(out=xn[:], in_=xn2[:], func=ACT.Sqrt, bias=tiny[:])
+            diagonal = work.tile([P, P], F32, name="diagonal")
+            nc.vector.scalar_tensor_tensor(
+                out=diagonal[:], in0=gram[:], scalar=0.5, in1=ident[:], op0=ALU.mult, op1=ALU.mult,
+                accum_out=half_norm2[b][:, first + r : first + r + 1],
+            )
+
+        def norms(b):
+            nc.scalar.activation(out=norm[b][:], in_=half_norm2[b][:], func=ACT.Sqrt, scale=2.0, bias=tiny[:])
+
+        def inverse_norms(b):
+            nc.vector.reciprocal(out=inv_norm[b][:], in_=norm[b][:])
+
+        def scale_inverse_norms(b):
+            nc.gpsimd.tensor_scalar(
+                out=w1_inv_qn[b][:], in0=inv_norm[b][:, ROW_TILES:], scalar1=w[:, 1:2], scalar2=0.0,
+                op0=ALU.mult, op1=ALU.add,
+            )
 
         def quantise(x_grouped, x_codes, x_scales):
             nc.vector.quantize_mx(
@@ -136,19 +187,19 @@ def tile_adaptiveattention_pb_kernel(tc, q_tanh, k_tanh, value, scoring_weights,
                 in_=x_grouped[:].rearrange("p c t -> p (c t)"),
             )
 
-        def spread(column, row_sb, copy):
+        def spread(columns, row_sb, copy):
             row = psum_t.tile([P, LK], F32, tag="t")
             for r in range(ROW_TILES):
                 nc.tensor.transpose(
-                    row[:, r * P : (r + 1) * P], column[:, r : r + 1].to_broadcast([P, P]), ident[:]
+                    row[:, r * P : (r + 1) * P], columns[:, r : r + 1].to_broadcast([P, P]), ident[:]
                 )
             copy(out=row_sb[:], in_=row[:])
 
         dot = {}
-        partial = {}
+        raw = {}
         cos_factor = {}
 
-        def dot_and_partial(t):
+        def dot_product(t):
             b, r = divmod(t, ROW_TILES)
             dot[t] = psum_mx.tile([P, LK], F32, tag="mx", name="dot")
             nc.tensor.matmul_mx(
@@ -160,26 +211,35 @@ def tile_adaptiveattention_pb_kernel(tc, q_tanh, k_tanh, value, scoring_weights,
                 start=True,
                 stop=True,
             )
-            partial[t] = batch.tile([P, LK], F32, name="partial")
+
+        def half_squared_distance(t):
+            b, r = divmod(t, ROW_TILES)
+            raw[t] = batch.tile([P, LK], F32, name="raw")
             nc.vector.scalar_tensor_tensor(
-                out=partial[t][:], in0=dot[t][:], scalar=-2.0, in1=kn2_row[b][:], op0=ALU.mult, op1=ALU.add
+                out=raw[t][:], in0=half_kn2_row[b][:], scalar=half_norm2[b][:, ROW_TILES + r : ROW_TILES + r + 1],
+                in1=dot[t][:], op0=ALU.add, op1=ALU.subtract,
             )
 
-        def squared_distance(t):
-            b, r = divmod(t, ROW_TILES)
-            nc.vector.tensor_scalar(
-                out=dist[t][:], in0=partial[t][:], scalar1=qn2[b][:, r : r + 1], scalar2=TINY, op0=ALU.add, op1=ALU.max
-            )
+        def clamp(t):
+            engine = nc.vector if t in CLAMP_ON_VECTOR else nc.gpsimd
+            engine.tensor_scalar(out=dist[t][:], in0=raw[t][:], scalar1=HUGE, scalar2=0.0, op0=ALU.min, op1=ALU.max)
 
         def square_root(t):
-            nc.scalar.activation(out=dist[t][:], in_=dist[t][:], func=ACT.Sqrt)
-
+            nc.scalar.activation(
+                out=dist[t][:], in_=dist[t][:], func=ACT.Sqrt, scale=twice_w2_squared[:], bias=tiny[:]
+            )
 
         def cosine_factor(t):
             b, r = divmod(t, ROW_TILES)
             cos_factor[t] = batch.tile([P, LK], F32, name="cos_factor")
+            if t in COS_ON_SCALAR:
+                nc.scalar.activation(
+                    out=cos_factor[t][:], in_=inv_kn_row[b][:], func=ACT.Identity,
+                    scale=w1_inv_qn[b][:, r : r + 1], bias=w[:, 0:1],
+                )
+                return
             nc.gpsimd.tensor_scalar(
-                out=cos_factor[t][:], in0=w1_inv_kn_row[b][:], scalar1=inv_qn[b][:, r : r + 1], scalar2=w[:, 0:1],
+                out=cos_factor[t][:], in0=inv_kn_row[b][:], scalar1=w1_inv_qn[b][:, r : r + 1], scalar2=w[:, 0:1],
                 op0=ALU.mult, op1=ALU.add,
             )
 
@@ -188,25 +248,26 @@ def tile_adaptiveattention_pb_kernel(tc, q_tanh, k_tanh, value, scoring_weights,
                 out=dot_cos[t][:], in0=cos_factor[t][:], scalar=cos_cap[:], in1=dot[t][:], op0=ALU.min, op1=ALU.mult
             )
 
-        def regroup_values(b):
-            for c in range(D // P):
-                cols = slice(c * P, (c + 1) * P)
-                nc.gpsimd.tensor_scalar(
-                    out=v_grouped[b][:, cols, :], in0=v_sb[b][:, :, cols].rearrange("p t d -> p d t"),
-                    scalar1=1.0, scalar2=0.0, op0=ALU.mult, op1=ALU.add,
-                )
+        def regroup_values(b, c):
+            cols = slice(c * P, (c + 1) * P)
+            nc.gpsimd.tensor_scalar(
+                out=v_grouped[b][:, cols, :], in0=v_sb[b][:, :, cols].rearrange("p t d -> p d t"),
+                scalar1=1.0, scalar2=0.0, op0=ALU.mult, op1=ALU.add,
+            )
 
         scores = {}
         prob = {}
+        attn = {}
         attn_t = {}
         a_grouped = {}
+        a_codes = {}
+        a_scales = {}
         product = {}
 
         def final_scores(t):
-            scores[t] = work.tile([P, LK], F32, name="scores")
-            nc.vector.scalar_tensor_tensor(
-                out=scores[t][:], in0=dist[t][:], scalar=neg_w2[:], in1=dot_cos[t][:], op0=ALU.mult, op1=ALU.add
-            )
+            scores[t] = scorep.tile([P, LK], F32, name="scores")
+            engine = nc.gpsimd if t in SCORES_ON_GPSIMD else nc.vector
+            engine.tensor_tensor(out=scores[t][:], in0=dot_cos[t][:], in1=dist[t][:], op=ALU.subtract)
 
         def row_maximum(t):
             nc.vector.tensor_reduce(
@@ -223,17 +284,17 @@ def tile_adaptiveattention_pb_kernel(tc, q_tanh, k_tanh, value, scoring_weights,
         def reciprocal_of_sum(t):
             nc.vector.reciprocal(out=inv_sum[:, t : t + 1], in_=exp_sum[:, t : t + 1])
 
-        def normalise_and_transpose(t):
-            attn = work.tile([P, LK], BF16)
-            if t >= N_TILES - LAST_ON_VECTOR:
-                nc.vector.tensor_scalar(
-                    out=attn[:], in0=prob[t][:], scalar1=inv_sum[:, t : t + 1], scalar2=None, op0=ALU.mult
-                )
-            else:
-                nc.gpsimd.tensor_scalar(
-                    out=attn[:], in0=prob[t][:], scalar1=inv_sum[:, t : t + 1], scalar2=0.0, op0=ALU.mult, op1=ALU.add
-                )
-            attn_words = attn[:].bitcast(F32)
+        def normalise(t):
+            attn[t] = work.tile([P, LK], BF16, name="attn")
+            if t in ON_SCALAR:
+                nc.scalar.activation(out=attn[t][:], in_=prob[t][:], func=ACT.Copy, scale=inv_sum[:, t : t + 1])
+                return
+            nc.vector.tensor_scalar(
+                out=attn[t][:], in0=prob[t][:], scalar1=inv_sum[:, t : t + 1], scalar2=None, op0=ALU.mult
+            )
+
+        def transpose_attention(t):
+            attn_words = attn[t][:].bitcast(F32)
             attn_t[t] = psum_t.tile([P, HALVES, P], F32, tag="t", name="attn_t")
             for u in range(HALVES):
                 nc.tensor.transpose(attn_t[t][:, u, :], attn_words[:, u * P : (u + 1) * P], ident[:])
@@ -242,95 +303,133 @@ def tile_adaptiveattention_pb_kernel(tc, q_tanh, k_tanh, value, scoring_weights,
             a_grouped[t] = work.tile([P, P, PACK], BF16, name="a_grouped", align_bytes=64)
             nc.scalar.copy(out=a_grouped[t][:].bitcast(F32), in_=attn_t[t][:].rearrange("p u i -> p i u"))
 
-        def quantise_and_multiply(t):
+        def quantise_attention(t):
+            a_codes[t] = work.tile([P, P], U32, name="a_codes", align_bytes=64)
+            a_scales[t] = work.tile([P, P], U8, name="a_scales", align_bytes=64)
+            quantise(a_grouped[t], a_codes[t], a_scales[t])
+
+        def multiply(t):
             b = t // ROW_TILES
-            a_codes = work.tile([P, P], U32, align_bytes=64)
-            a_scales = work.tile([P, P], U8, align_bytes=64)
-            quantise(a_grouped[t], a_codes, a_scales)
             product[t] = psum_mx.tile([P, D], F32, tag="mx", name="product")
             nc.tensor.matmul_mx(
                 out=product[t][:],
-                lhsT=a_codes[:].bitcast(FP8X4),
-                lhsT_scale=a_scales[:],
+                lhsT=a_codes[t][:].bitcast(FP8X4),
+                lhsT_scale=a_scales[t][:],
                 rhs=v_codes[b][:].bitcast(FP8X4),
                 rhs_scale=v_scales[b][:],
                 start=True,
                 stop=True,
             )
 
-        def store(t):
+        def store(t, copy):
             b, r = divmod(t, ROW_TILES)
-            result = work.tile([P, D], F32)
-            nc.scalar.copy(out=result[:], in_=product[t][:])
+            result = results.tile([P, D], F32, name="result")
+            copy(out=result[:], in_=product[t][:])
             nc.sync.dma_start(out=out[b].rearrange("(p r) d -> p r d", r=ROW_TILES)[:, r, :], in_=result[:])
 
-        def vector_scaled_by_w1(out, in_):
-            nc.vector.tensor_scalar(out=out, in0=in_, scalar1=w[:, 1:2], scalar2=None, op0=ALU.mult)
-
-        def scalar_scaled_by_w1(out, in_):
-            nc.scalar.activation(out=out, in_=in_, func=ACT.Copy, scale=w[:, 1:2])
-
-        def products(b, scaled_by_w1):
-            first = b * ROW_TILES
-            half = first + ROW_TILES // 2
-            for t in range(first, half):
-                dot_and_partial(t)
-            spread(inv_kn[b], w1_inv_kn_row[b], scaled_by_w1)
-            nc.vector.reciprocal(out=inv_qn[b][:], in_=qn[b][:])
-            for t in range(half, first + ROW_TILES):
-                dot_and_partial(t)
-            for t in range(first, first + ROW_TILES):
-                cosine_factor(t)
-
-        regroup_values(0)
-        group_features(transpose_features(k_sb[0]), k_grouped[0], nc.vector.tensor_copy)
-        group_features(transpose_features(q_sb[0]), q_grouped[0], nc.vector.tensor_copy)
-        norms(k_sb[0], k_squares[0], kn2[0], kn[0])
+        vcopy, acopy = nc.vector.tensor_copy, nc.scalar.copy
+        K, Q = 0, ROW_TILES
+        SCORES_ON_GPSIMD = ()
+        CLAMP_ON_VECTOR = ()
+        ON_SCALAR = (0, 1, 2, 3)
+        COS_ON_SCALAR = ()
+        mixing_weights()
+        k0 = transpose_features(k_sb[0])
+        q0 = transpose_features(q_sb[0])
+        for c in range(D // P):
+            regroup_values(0, c)
+        for r in range(ROW_TILES):
+            square(k_sb[0], 0, K, r)
+        for pair in range(2):
+            group_features(k0, pair, k_grouped[0], vcopy)
         quantise(k_grouped[0], k_codes[0], k_scales[0])
+        for pair in range(2):
+            group_features(q0, pair, q_grouped[0], vcopy)
+        spread(half_norm2[0], half_kn2_row[0], acopy)
         quantise(q_grouped[0], q_codes[0], q_scales[0])
-        spread(kn2[0], kn2_row[0], nc.vector.tensor_copy)
-        nc.vector.reciprocal(out=inv_kn[0][:], in_=kn[0][:])
-        norms(q_sb[0], q_squares[0], qn2[0], qn[0])
-        k1_banks = transpose_features(k_sb[1])
-        products(0, vector_scaled_by_w1)
-        regroup_values(1)
-        group_features(k1_banks, k_grouped[1], nc.scalar.copy)
-        q1_banks = transpose_features(q_sb[1])
-        norms(k_sb[1], k_squares[1], kn2[1], kn[1])
-        group_features(q1_banks, q_grouped[1], nc.scalar.copy)
-        spread(kn2[1], kn2_row[1], nc.scalar.copy)
-        norms(q_sb[1], q_squares[1], qn2[1], qn[1])
-        for t in range(ROW_TILES):
-            dot_and_cosine(t)
-        nc.vector.reciprocal(out=inv_kn[1][:], in_=kn[1][:])
+        for r in range(ROW_TILES):
+            square(q_sb[0], 0, Q, r)
+        k1 = transpose_features(k_sb[1])
+        for t in range(4):
+            dot_product(t)
+        group_features(k1, 0, k_grouped[1], vcopy)
+        norms(0)
+        group_features(k1, 1, k_grouped[1], acopy)
+        for t in range(4):
+            half_squared_distance(t)
+            clamp(t)
+            if t == 1:
+                inverse_norms(0)
+                scale_inverse_norms(0)
+        square(k_sb[1], 1, K, 0)
+        spread(inv_norm[0], inv_kn_row[0], acopy)
+        for t in range(4):
+            cosine_factor(t)
+        q1 = transpose_features(q_sb[1])
+        for r in range(1, ROW_TILES):
+            square(k_sb[1], 1, K, r)
         quantise(k_grouped[1], k_codes[1], k_scales[1])
+        for pair in range(2):
+            group_features(q1, pair, q_grouped[1], vcopy)
         quantise(q_grouped[1], q_codes[1], q_scales[1])
-        for t in range(ROW_TILES):
-            squared_distance(t)
-        for t in range(ROW_TILES):
+        square(q_sb[1], 1, Q, 0)
+        spread(half_norm2[1], half_kn2_row[1], acopy)
+        for r in range(1, ROW_TILES):
+            square(q_sb[1], 1, Q, r)
+        square_root(0)
+        norms(1)
+        for t in range(4):
+            dot_and_cosine(t)
+        inverse_norms(1)
+        dot_product(4)
+        dot_product(5)
+        spread(inv_norm[1], inv_kn_row[1], acopy)
+        for t in range(6, 8):
+            dot_product(t)
+        for t in range(4, 9):
+            if t < 8:
+                half_squared_distance(t)
+            if t > 4:
+                clamp(t - 1)
+        for t in range(1, 4):
             square_root(t)
-        products(1, scalar_scaled_by_w1)
-        for t in range(ROW_TILES, N_TILES):
-            squared_distance(t)
+        for t in range(4, 8):
             square_root(t)
-        for step in range(N_TILES + 5):
-            if 0 <= step - 3 < N_TILES:
-                group_attention(step - 3)
-            if 0 <= step - 1 < N_TILES:
-                exponentials(step - 1)
-            if 0 <= step - 2 < N_TILES:
-                reciprocal_of_sum(step - 2)
+        scale_inverse_norms(1)
+        for t in range(4, 8):
+            if t not in COS_ON_SCALAR:
+                cosine_factor(t)
+        for c in range(D // P):
+            regroup_values(1, c)
+        LEAD = 4
+        done = []
+        tail = 0
+        for step in range(N_TILES + 8):
+            seconds = []
+            if step >= LEAD:
+                seconds = list(range(tail, min(N_TILES, tail + (1 if step == LEAD else 2))))
+                tail += len(seconds)
             if step < N_TILES:
                 final_scores(step)
-            if 0 <= step - 2 < N_TILES:
-                normalise_and_transpose(step - 2)
-            if 0 <= step - 5 < N_TILES:
-                store(step - 5)
-            if 0 <= step - 4 < N_TILES:
-                quantise_and_multiply(step - 4)
-            if step < ROW_TILES:
-                dot_and_cosine(ROW_TILES + step)
+            for t in seconds:
+                reciprocal_of_sum(t)
+            for t in done:
+                quantise_attention(t)
+                multiply(t)
+            if ROW_TILES <= step + 2 < N_TILES:
+                dot_and_cosine(step + 2)
+            for t in seconds:
+                normalise(t)
+                transpose_attention(t)
             if step < N_TILES:
                 row_maximum(step)
-            if step < B:
-                quantise(v_grouped[step], v_codes[step], v_scales[step])
+                exponentials(step)
+            for t in seconds:
+                group_attention(t)
+            for t in done:
+                store(t, acopy)
+            done = seconds
+            if step == 4:
+                quantise(v_grouped[0], v_codes[0], v_scales[0])
+            if step == 6:
+                quantise(v_grouped[1], v_codes[1], v_scales[1])

@@ -31,9 +31,9 @@ def tile_adaptiveattention_pb_kernel(tc, q_tanh, k_tanh, value, scoring_weights,
     nc = tc.nc
     with ExitStack() as ctx:
         keep = ctx.enter_context(tc.tile_pool(name="keep", bufs=1))
-        batch = ctx.enter_context(tc.tile_pool(name="batch", bufs=ROW_TILES))
-        work = ctx.enter_context(tc.tile_pool(name="work", bufs=4))
-        scorep = ctx.enter_context(tc.tile_pool(name="scorep", bufs=6))
+        batch = ctx.enter_context(tc.tile_pool(name="batch", bufs=N_TILES))
+        work = ctx.enter_context(tc.tile_pool(name="work", bufs=N_TILES))
+        scorep = ctx.enter_context(tc.tile_pool(name="scorep", bufs=N_TILES))
         results = ctx.enter_context(tc.tile_pool(name="results", bufs=N_TILES))
         psum_t = ctx.enter_context(tc.psum_pool(name="psum_t", bufs=4))
         psum_mx = ctx.enter_context(tc.psum_pool(name="psum_mx", bufs=4))
@@ -72,7 +72,6 @@ def tile_adaptiveattention_pb_kernel(tc, q_tanh, k_tanh, value, scoring_weights,
 
         nc.vector.memset(w_raw[:], 0.0)
         nc.vector.memset(tiny[:], TINY)
-        nc.scalar.dma_start(out=w_raw[0:1, 0:3], in_=scoring_weights.unsqueeze(0))
         nc.scalar.activation(out=tiny_root[:], in_=tiny[:], func=ACT.Sqrt)
         make_identity(nc, ident[:])
         nc.gpsimd.memset(ones[:], 1.0)
@@ -92,6 +91,8 @@ def tile_adaptiveattention_pb_kernel(tc, q_tanh, k_tanh, value, scoring_weights,
                 nc.sync.dma_start(
                     out=q_sb[b][:, i * tiles : (i + 1) * tiles, :], in_=q_rows[:, i * tiles : (i + 1) * tiles, :]
                 )
+            if b == 0:
+                nc.sync.dma_start(out=w_raw[0:1, 0:3], in_=scoring_weights.unsqueeze(0))
             nc.sync.dma_start(
                 out=v_sb[b][:].rearrange("p (u e) d -> p u (e d)", u=HALVES),
                 in_=value[b].rearrange("(u p e) d -> p u (e d)", u=HALVES, p=P),
@@ -221,17 +222,25 @@ def tile_adaptiveattention_pb_kernel(tc, q_tanh, k_tanh, value, scoring_weights,
             )
 
         def clamp(t):
-            engine = nc.vector if t in CLAMP_ON_VECTOR else nc.gpsimd
-            engine.tensor_scalar(out=dist[t][:], in0=raw[t][:], scalar1=HUGE, scalar2=0.0, op0=ALU.min, op1=ALU.max)
+            if t in CLAMP_ON_VECTOR:
+                nc.vector.tensor_scalar(out=raw[t][:], in0=raw[t][:], scalar1=0.0, scalar2=HUGE, op0=ALU.max, op1=ALU.min)
+            else:
+                nc.gpsimd.tensor_scalar(out=raw[t][:], in0=raw[t][:], scalar1=HUGE, scalar2=0.0, op0=ALU.min, op1=ALU.max)
 
         def square_root(t):
             nc.scalar.activation(
-                out=dist[t][:], in_=dist[t][:], func=ACT.Sqrt, scale=twice_w2_squared[:], bias=tiny[:]
+                out=dist[t][:], in_=raw[t][:], func=ACT.Sqrt, scale=twice_w2_squared[:], bias=tiny[:]
             )
 
         def cosine_factor(t):
             b, r = divmod(t, ROW_TILES)
             cos_factor[t] = batch.tile([P, LK], F32, name="cos_factor")
+            if t in COS_ON_VECTOR:
+                nc.vector.tensor_scalar(
+                    out=cos_factor[t][:], in0=inv_kn_row[b][:], scalar1=w1_inv_qn[b][:, r : r + 1], scalar2=w[:, 0:1],
+                    op0=ALU.mult, op1=ALU.add,
+                )
+                return
             if t in COS_ON_SCALAR:
                 nc.scalar.activation(
                     out=cos_factor[t][:], in_=inv_kn_row[b][:], func=ACT.Identity,
@@ -249,7 +258,8 @@ def tile_adaptiveattention_pb_kernel(tc, q_tanh, k_tanh, value, scoring_weights,
             )
 
         def regroup_values(b, c):
-            cols = slice(c * P, (c + 1) * P)
+            width = D // PIECES
+            cols = slice(c * width, (c + 1) * width)
             nc.gpsimd.tensor_scalar(
                 out=v_grouped[b][:, cols, :], in0=v_sb[b][:, :, cols].rearrange("p t d -> p d t"),
                 scalar1=1.0, scalar2=0.0, op0=ALU.mult, op1=ALU.add,
@@ -266,8 +276,7 @@ def tile_adaptiveattention_pb_kernel(tc, q_tanh, k_tanh, value, scoring_weights,
 
         def final_scores(t):
             scores[t] = scorep.tile([P, LK], F32, name="scores")
-            engine = nc.gpsimd if t in SCORES_ON_GPSIMD else nc.vector
-            engine.tensor_tensor(out=scores[t][:], in0=dot_cos[t][:], in1=dist[t][:], op=ALU.subtract)
+            nc.vector.tensor_tensor(out=scores[t][:], in0=dot_cos[t][:], in1=dist[t][:], op=ALU.subtract)
 
         def row_maximum(t):
             nc.vector.tensor_reduce(
@@ -329,81 +338,94 @@ def tile_adaptiveattention_pb_kernel(tc, q_tanh, k_tanh, value, scoring_weights,
 
         vcopy, acopy = nc.vector.tensor_copy, nc.scalar.copy
         K, Q = 0, ROW_TILES
-        SCORES_ON_GPSIMD = ()
-        CLAMP_ON_VECTOR = ()
+        PIECES = 4
         ON_SCALAR = (0, 1, 2, 3)
-        COS_ON_SCALAR = ()
-        mixing_weights()
+        COS_ON_SCALAR = (4, 5, 6, 7)
+        COS_ON_VECTOR = ()
+        CLAMP_ON_VECTOR = tuple(range(N_TILES))
         k0 = transpose_features(k_sb[0])
         q0 = transpose_features(q_sb[0])
-        for c in range(D // P):
-            regroup_values(0, c)
         for r in range(ROW_TILES):
             square(k_sb[0], 0, K, r)
         for pair in range(2):
             group_features(k0, pair, k_grouped[0], vcopy)
         quantise(k_grouped[0], k_codes[0], k_scales[0])
+        for c in range(PIECES):
+            regroup_values(0, c)
         for pair in range(2):
             group_features(q0, pair, q_grouped[0], vcopy)
+        for r in range(2):
+            square(q_sb[0], 0, Q, r)
         spread(half_norm2[0], half_kn2_row[0], acopy)
         quantise(q_grouped[0], q_codes[0], q_scales[0])
-        for r in range(ROW_TILES):
+        mixing_weights()
+        for r in range(2, ROW_TILES):
             square(q_sb[0], 0, Q, r)
         k1 = transpose_features(k_sb[1])
         for t in range(4):
             dot_product(t)
         group_features(k1, 0, k_grouped[1], vcopy)
-        norms(0)
         group_features(k1, 1, k_grouped[1], acopy)
-        for t in range(4):
-            half_squared_distance(t)
-            clamp(t)
+        norms(0)
+        for t in range(5):
+            if t < 4:
+                half_squared_distance(t)
+            if t > 0:
+                clamp(t - 1)
             if t == 1:
                 inverse_norms(0)
                 scale_inverse_norms(0)
-        square(k_sb[1], 1, K, 0)
+        for r in range(2):
+            square(k_sb[1], 1, K, r)
         spread(inv_norm[0], inv_kn_row[0], acopy)
         for t in range(4):
             cosine_factor(t)
         q1 = transpose_features(q_sb[1])
-        for r in range(1, ROW_TILES):
+        for r in range(2, ROW_TILES - 0):
             square(k_sb[1], 1, K, r)
+        for r in range(ROW_TILES - 0, ROW_TILES):
+            squares_on_tensor(k_grouped[1], 1, K, r)
         quantise(k_grouped[1], k_codes[1], k_scales[1])
-        for pair in range(2):
-            group_features(q1, pair, q_grouped[1], vcopy)
-        quantise(q_grouped[1], q_codes[1], q_scales[1])
-        square(q_sb[1], 1, Q, 0)
-        spread(half_norm2[1], half_kn2_row[1], acopy)
-        for r in range(1, ROW_TILES):
+        group_features(q1, 0, q_grouped[1], acopy)
+        group_features(q1, 1, q_grouped[1], acopy)
+        for r in range(min(1, ROW_TILES - 0)):
             square(q_sb[1], 1, Q, r)
+        spread(half_norm2[1], half_kn2_row[1], acopy)
+        for r in range(1, ROW_TILES - 0):
+            square(q_sb[1], 1, Q, r)
+        dot_and_cosine(0)
+        quantise(q_grouped[1], q_codes[1], q_scales[1])
+        dot_and_cosine(1)
+        for r in range(ROW_TILES - 0, ROW_TILES):
+            squares_on_tensor(q_grouped[1], 1, Q, r)
+        for t in range(2, 4):
+            dot_and_cosine(t)
         square_root(0)
         norms(1)
-        for t in range(4):
-            dot_and_cosine(t)
-        inverse_norms(1)
+        for t in range(1, 4):
+            square_root(t)
+        for c in range(PIECES):
+            regroup_values(1, c)
         dot_product(4)
         dot_product(5)
-        spread(inv_norm[1], inv_kn_row[1], acopy)
-        for t in range(6, 8):
-            dot_product(t)
         for t in range(4, 9):
+            if t == 5:
+                inverse_norms(1)
+                spread(inv_norm[1], inv_kn_row[1], acopy)
+            if 5 < t < 8:
+                dot_product(t)
             if t < 8:
                 half_squared_distance(t)
             if t > 4:
                 clamp(t - 1)
-        for t in range(1, 4):
-            square_root(t)
-        for t in range(4, 8):
-            square_root(t)
         scale_inverse_norms(1)
         for t in range(4, 8):
-            if t not in COS_ON_SCALAR:
-                cosine_factor(t)
-        for c in range(D // P):
-            regroup_values(1, c)
+            square_root(t)
         LEAD = 4
         done = []
         tail = 0
+        for t in (4, 5):
+            cosine_factor(t)
         for step in range(N_TILES + 8):
             seconds = []
             if step >= LEAD:
@@ -411,23 +433,25 @@ def tile_adaptiveattention_pb_kernel(tc, q_tanh, k_tanh, value, scoring_weights,
                 tail += len(seconds)
             if step < N_TILES:
                 final_scores(step)
+            if step in {1: 6, 2: 7}:
+                cosine_factor({1: 6, 2: 7}[step])
             for t in seconds:
                 reciprocal_of_sum(t)
-            for t in done:
-                quantise_attention(t)
-                multiply(t)
-            if ROW_TILES <= step + 2 < N_TILES:
+            if step < N_TILES and ROW_TILES <= step + 2 < N_TILES:
                 dot_and_cosine(step + 2)
             for t in seconds:
                 normalise(t)
                 transpose_attention(t)
+            for t in done:
+                quantise_attention(t)
+                multiply(t)
             if step < N_TILES:
                 row_maximum(step)
                 exponentials(step)
             for t in seconds:
                 group_attention(t)
             for t in done:
-                store(t, acopy)
+                store(t, vcopy if t in () else acopy)
             done = seconds
             if step == 4:
                 quantise(v_grouped[0], v_codes[0], v_scales[0])

@@ -31,9 +31,8 @@ def tile_adaptiveattention_pb_kernel(tc, q_tanh, k_tanh, value, scoring_weights,
     nc = tc.nc
     with ExitStack() as ctx:
         keep = ctx.enter_context(tc.tile_pool(name="keep", bufs=1))
-        batch = ctx.enter_context(tc.tile_pool(name="batch", bufs=N_TILES))
+        batch = ctx.enter_context(tc.tile_pool(name="batch", bufs=ROW_TILES))
         work = ctx.enter_context(tc.tile_pool(name="work", bufs=N_TILES))
-        scorep = ctx.enter_context(tc.tile_pool(name="scorep", bufs=N_TILES))
         results = ctx.enter_context(tc.tile_pool(name="results", bufs=N_TILES))
         psum_t = ctx.enter_context(tc.psum_pool(name="psum_t", bufs=4))
         psum_mx = ctx.enter_context(tc.psum_pool(name="psum_mx", bufs=4))
@@ -59,8 +58,9 @@ def tile_adaptiveattention_pb_kernel(tc, q_tanh, k_tanh, value, scoring_weights,
         w1_inv_qn = [keep.tile([P, ROW_TILES], F32, name="w1_inv_qn%d" % b) for b in range(B)]
         half_kn2_row = [keep.tile([P, LK], F32, name="half_kn2_row%d" % b) for b in range(B)]
         inv_kn_row = [keep.tile([P, LK], F32, name="inv_kn_row%d" % b) for b in range(B)]
-        dot_cos = [keep.tile([P, LK], F32, name="dot_cos%d" % t) for t in range(N_TILES)]
-        dist = [keep.tile([P, LK], F32, name="dist%d" % t) for t in range(N_TILES)]
+        dot_cos = keep.tile([P, N_TILES, LK], F32)
+        dist = keep.tile([P, N_TILES, LK], F32)
+        scores = keep.tile([P, N_TILES, LK], F32)
         neg_max = keep.tile([P, N_TILES], F32)
         exp_sum = keep.tile([P, N_TILES], F32)
         inv_sum = keep.tile([P, N_TILES], F32)
@@ -197,7 +197,6 @@ def tile_adaptiveattention_pb_kernel(tc, q_tanh, k_tanh, value, scoring_weights,
             copy(out=row_sb[:], in_=row[:])
 
         dot = {}
-        raw = {}
         cos_factor = {}
 
         def dot_product(t):
@@ -215,22 +214,18 @@ def tile_adaptiveattention_pb_kernel(tc, q_tanh, k_tanh, value, scoring_weights,
 
         def half_squared_distance(t):
             b, r = divmod(t, ROW_TILES)
-            raw[t] = batch.tile([P, LK], F32, name="raw")
             nc.vector.scalar_tensor_tensor(
-                out=raw[t][:], in0=half_kn2_row[b][:], scalar=half_norm2[b][:, ROW_TILES + r : ROW_TILES + r + 1],
+                out=dist[:, t, :], in0=half_kn2_row[b][:], scalar=half_norm2[b][:, ROW_TILES + r : ROW_TILES + r + 1],
                 in1=dot[t][:], op0=ALU.add, op1=ALU.subtract,
             )
 
-        def clamp(t):
-            if t in CLAMP_ON_VECTOR:
-                nc.vector.tensor_scalar(out=raw[t][:], in0=raw[t][:], scalar1=0.0, scalar2=HUGE, op0=ALU.max, op1=ALU.min)
-            else:
-                nc.gpsimd.tensor_scalar(out=raw[t][:], in0=raw[t][:], scalar1=HUGE, scalar2=0.0, op0=ALU.min, op1=ALU.max)
+        def clamp(first, n):
+            tiles = dist[:, first : first + n, :]
+            nc.vector.tensor_scalar(out=tiles, in0=tiles, scalar1=0.0, scalar2=HUGE, op0=ALU.max, op1=ALU.min)
 
-        def square_root(t):
-            nc.scalar.activation(
-                out=dist[t][:], in_=raw[t][:], func=ACT.Sqrt, scale=twice_w2_squared[:], bias=tiny[:]
-            )
+        def square_roots(first, n):
+            tiles = dist[:, first : first + n, :]
+            nc.scalar.activation(out=tiles, in_=tiles, func=ACT.Sqrt, scale=twice_w2_squared[:], bias=tiny[:])
 
         def cosine_factor(t):
             b, r = divmod(t, ROW_TILES)
@@ -254,7 +249,7 @@ def tile_adaptiveattention_pb_kernel(tc, q_tanh, k_tanh, value, scoring_weights,
 
         def dot_and_cosine(t):
             nc.vector.scalar_tensor_tensor(
-                out=dot_cos[t][:], in0=cos_factor[t][:], scalar=cos_cap[:], in1=dot[t][:], op0=ALU.min, op1=ALU.mult
+                out=dot_cos[:, t, :], in0=cos_factor[t][:], scalar=cos_cap[:], in1=dot[t][:], op0=ALU.min, op1=ALU.mult
             )
 
         def regroup_values(b, c):
@@ -265,7 +260,6 @@ def tile_adaptiveattention_pb_kernel(tc, q_tanh, k_tanh, value, scoring_weights,
                 scalar1=1.0, scalar2=0.0, op0=ALU.mult, op1=ALU.add,
             )
 
-        scores = {}
         prob = {}
         attn = {}
         attn_t = {}
@@ -274,24 +268,28 @@ def tile_adaptiveattention_pb_kernel(tc, q_tanh, k_tanh, value, scoring_weights,
         a_scales = {}
         product = {}
 
-        def final_scores(t):
-            scores[t] = scorep.tile([P, LK], F32, name="scores")
-            nc.vector.tensor_tensor(out=scores[t][:], in0=dot_cos[t][:], in1=dist[t][:], op=ALU.subtract)
+        def final_scores(first, n):
+            tiles = slice(first, first + n)
+            nc.vector.tensor_tensor(
+                out=scores[:, tiles, :], in0=dot_cos[:, tiles, :], in1=dist[:, tiles, :], op=ALU.subtract
+            )
 
-        def row_maximum(t):
+        def row_maxima(first, n):
+            tiles = slice(first, first + n)
             nc.vector.tensor_reduce(
-                out=neg_max[:, t : t + 1], in_=scores[t][:], axis=AXIS.X, op=ALU.max, negate=True
+                out=neg_max[:, tiles], in_=scores[:, tiles, :], axis=AXIS.X, op=ALU.max, negate=True
             )
 
         def exponentials(t):
             prob[t] = work.tile([P, LK], F32, name="prob")
             nc.scalar.activation(
-                out=prob[t][:], in_=scores[t][:], func=ACT.Exp, bias=neg_max[:, t : t + 1],
+                out=prob[t][:], in_=scores[:, t, :], func=ACT.Exp, bias=neg_max[:, t : t + 1],
                 accum_out=exp_sum[:, t : t + 1],
             )
 
-        def reciprocal_of_sum(t):
-            nc.vector.reciprocal(out=inv_sum[:, t : t + 1], in_=exp_sum[:, t : t + 1])
+        def reciprocals_of_sums(first, n):
+            tiles = slice(first, first + n)
+            nc.vector.reciprocal(out=inv_sum[:, tiles], in_=exp_sum[:, tiles])
 
         def normalise(t):
             attn[t] = work.tile([P, LK], BF16, name="attn")
@@ -302,47 +300,56 @@ def tile_adaptiveattention_pb_kernel(tc, q_tanh, k_tanh, value, scoring_weights,
                 out=attn[t][:], in0=prob[t][:], scalar1=inv_sum[:, t : t + 1], scalar2=None, op0=ALU.mult
             )
 
-        def transpose_attention(t):
-            attn_words = attn[t][:].bitcast(F32)
-            attn_t[t] = psum_t.tile([P, HALVES, P], F32, tag="t", name="attn_t")
-            for u in range(HALVES):
-                nc.tensor.transpose(attn_t[t][:, u, :], attn_words[:, u * P : (u + 1) * P], ident[:])
+        def transpose_attention(first, n):
+            attn_t[first] = psum_t.tile([P, n, HALVES, P], F32, tag="t", name="attn_t")
+            for i in range(n):
+                attn_words = attn[first + i][:].bitcast(F32)
+                for u in range(HALVES):
+                    nc.tensor.transpose(attn_t[first][:, i, u, :], attn_words[:, u * P : (u + 1) * P], ident[:])
 
-        def group_attention(t):
-            a_grouped[t] = work.tile([P, P, PACK], BF16, name="a_grouped", align_bytes=64)
-            nc.scalar.copy(out=a_grouped[t][:].bitcast(F32), in_=attn_t[t][:].rearrange("p u i -> p i u"))
-
-        def quantise_attention(t):
-            a_codes[t] = work.tile([P, P], U32, name="a_codes", align_bytes=64)
-            a_scales[t] = work.tile([P, P], U8, name="a_scales", align_bytes=64)
-            quantise(a_grouped[t], a_codes[t], a_scales[t])
-
-        def multiply(t):
-            b = t // ROW_TILES
-            product[t] = psum_mx.tile([P, D], F32, tag="mx", name="product")
-            nc.tensor.matmul_mx(
-                out=product[t][:],
-                lhsT=a_codes[t][:].bitcast(FP8X4),
-                lhsT_scale=a_scales[t][:],
-                rhs=v_codes[b][:].bitcast(FP8X4),
-                rhs_scale=v_scales[b][:],
-                start=True,
-                stop=True,
+        def group_attention(first, n):
+            a_grouped[first] = work.tile([P, n * P, PACK], BF16, name="a_grouped%d" % n, align_bytes=64)
+            nc.scalar.copy(
+                out=a_grouped[first][:].bitcast(F32).rearrange("p (t i) u -> p t i u", t=n),
+                in_=attn_t[first][:].rearrange("p t u i -> p t i u"),
             )
 
-        def store(t, copy):
+        def quantise_attention(first, n):
+            codes = work.tile([P, n * P], U32, name="a_codes%d" % n, align_bytes=64)
+            scales = work.tile([P, n * P], U8, name="a_scales%d" % n, align_bytes=64)
+            quantise(a_grouped[first], codes, scales)
+            for i in range(n):
+                a_codes[first + i] = codes[:, i * P : (i + 1) * P]
+                a_scales[first + i] = scales[:, i * P : (i + 1) * P]
+
+        def multiply(t, parts=1):
+            b = t // ROW_TILES
+            for i in range(parts):
+                cols = slice(i * D // parts, (i + 1) * D // parts)
+                product[t, i] = psum_mx.tile([P, D // parts], F32, tag="mx", name="product")
+                nc.tensor.matmul_mx(
+                    out=product[t, i][:],
+                    lhsT=a_codes[t].bitcast(FP8X4),
+                    lhsT_scale=a_scales[t],
+                    rhs=v_codes[b][:, cols].bitcast(FP8X4),
+                    rhs_scale=v_scales[b][:, cols],
+                    start=True,
+                    stop=True,
+                )
+
+        def store(t, copy, part=0, parts=1):
             b, r = divmod(t, ROW_TILES)
-            result = results.tile([P, D], F32, name="result")
-            copy(out=result[:], in_=product[t][:])
-            nc.sync.dma_start(out=out[b].rearrange("(p r) d -> p r d", r=ROW_TILES)[:, r, :], in_=result[:])
+            cols = slice(part * D // parts, (part + 1) * D // parts)
+            result = results.tile([P, D // parts], F32, name="result")
+            copy(out=result[:], in_=product[t, part][:])
+            nc.sync.dma_start(out=out[b].rearrange("(p r) d -> p r d", r=ROW_TILES)[:, r, cols], in_=result[:])
 
         vcopy, acopy = nc.vector.tensor_copy, nc.scalar.copy
         K, Q = 0, ROW_TILES
         PIECES = 4
-        ON_SCALAR = (0, 1, 2, 3)
+        ON_SCALAR = (0, 1)
         COS_ON_SCALAR = (4, 5, 6, 7)
         COS_ON_VECTOR = ()
-        CLAMP_ON_VECTOR = tuple(range(N_TILES))
         k0 = transpose_features(k_sb[0])
         q0 = transpose_features(q_sb[0])
         for r in range(ROW_TILES):
@@ -367,93 +374,123 @@ def tile_adaptiveattention_pb_kernel(tc, q_tanh, k_tanh, value, scoring_weights,
         group_features(k1, 0, k_grouped[1], vcopy)
         group_features(k1, 1, k_grouped[1], acopy)
         norms(0)
-        for t in range(5):
-            if t < 4:
-                half_squared_distance(t)
-            if t > 0:
-                clamp(t - 1)
-            if t == 1:
-                inverse_norms(0)
-                scale_inverse_norms(0)
-        for r in range(2):
+        half_squared_distance(0)
+        half_squared_distance(1)
+        inverse_norms(0)
+        scale_inverse_norms(0)
+        half_squared_distance(2)
+        clamp(0, 2)
+        half_squared_distance(3)
+        for r in range(3):
             square(k_sb[1], 1, K, r)
         spread(inv_norm[0], inv_kn_row[0], acopy)
         for t in range(4):
             cosine_factor(t)
         q1 = transpose_features(q_sb[1])
-        for r in range(2, ROW_TILES - 0):
+        for r in range(3, ROW_TILES - 0):
             square(k_sb[1], 1, K, r)
         for r in range(ROW_TILES - 0, ROW_TILES):
             squares_on_tensor(k_grouped[1], 1, K, r)
         quantise(k_grouped[1], k_codes[1], k_scales[1])
+        clamp(2, 2)
         group_features(q1, 0, q_grouped[1], acopy)
-        group_features(q1, 1, q_grouped[1], acopy)
-        for r in range(min(1, ROW_TILES - 0)):
-            square(q_sb[1], 1, Q, r)
+        group_features(q1, 1, q_grouped[1], vcopy)
+        square(q_sb[1], 1, Q, 0)
         spread(half_norm2[1], half_kn2_row[1], acopy)
         for r in range(1, ROW_TILES - 0):
             square(q_sb[1], 1, Q, r)
         dot_and_cosine(0)
         quantise(q_grouped[1], q_codes[1], q_scales[1])
-        dot_and_cosine(1)
+        for t in range(1, 3):
+            dot_and_cosine(t)
         for r in range(ROW_TILES - 0, ROW_TILES):
             squares_on_tensor(q_grouped[1], 1, Q, r)
-        for t in range(2, 4):
-            dot_and_cosine(t)
-        square_root(0)
+        dot_and_cosine(3)
         norms(1)
-        for t in range(1, 4):
-            square_root(t)
+        square_roots(0, 2)
+        square_roots(2, 2)
         for c in range(PIECES):
             regroup_values(1, c)
-        dot_product(4)
-        dot_product(5)
-        for t in range(4, 9):
-            if t == 5:
-                inverse_norms(1)
-                spread(inv_norm[1], inv_kn_row[1], acopy)
-            if 5 < t < 8:
-                dot_product(t)
-            if t < 8:
-                half_squared_distance(t)
-            if t > 4:
-                clamp(t - 1)
-        scale_inverse_norms(1)
         for t in range(4, 8):
-            square_root(t)
-        LEAD = 4
-        done = []
-        tail = 0
+            dot_product(t)
+        half_squared_distance(4)
+        inverse_norms(1)
+        scale_inverse_norms(1)
+        spread(inv_norm[1], inv_kn_row[1], acopy)
+        half_squared_distance(5)
+        half_squared_distance(6)
+        clamp(4, 2)
+        half_squared_distance(7)
+        final_scores(0, 1)
+        clamp(6, 2)
+        final_scores(1, 1)
+        square_roots(4, 2)
+
+        square_roots(6, 2)
         for t in (4, 5):
             cosine_factor(t)
-        for step in range(N_TILES + 8):
-            seconds = []
-            if step >= LEAD:
-                seconds = list(range(tail, min(N_TILES, tail + (1 if step == LEAD else 2))))
-                tail += len(seconds)
-            if step < N_TILES:
-                final_scores(step)
-            if step in {1: 6, 2: 7}:
-                cosine_factor({1: 6, 2: 7}[step])
-            for t in seconds:
-                reciprocal_of_sum(t)
-            if step < N_TILES and ROW_TILES <= step + 2 < N_TILES:
-                dot_and_cosine(step + 2)
-            for t in seconds:
-                normalise(t)
-                transpose_attention(t)
-            for t in done:
-                quantise_attention(t)
-                multiply(t)
-            if step < N_TILES:
-                row_maximum(step)
-                exponentials(step)
-            for t in seconds:
-                group_attention(t)
-            for t in done:
-                store(t, vcopy if t in () else acopy)
-            done = seconds
-            if step == 4:
-                quantise(v_grouped[0], v_codes[0], v_scales[0])
-            if step == 6:
-                quantise(v_grouped[1], v_codes[1], v_scales[1])
+        row_maxima(0, 2)
+        exponentials(0)
+        exponentials(1)
+        cosine_factor(6)
+        final_scores(2, 2)
+        dot_and_cosine(4)
+        dot_and_cosine(5)
+        row_maxima(2, 2)
+        exponentials(2)
+        cosine_factor(7)
+        exponentials(3)
+        quantise(v_grouped[0], v_codes[0], v_scales[0])
+        final_scores(4, 2)
+        reciprocals_of_sums(0, 2)
+        dot_and_cosine(6)
+        row_maxima(4, 2)
+        for t in (0, 1):
+            normalise(t)
+        transpose_attention(0, 2)
+        exponentials(4)
+        exponentials(5)
+        group_attention(0, 2)
+        dot_and_cosine(7)
+        final_scores(6, 2)
+        reciprocals_of_sums(2, 2)
+        row_maxima(6, 2)
+        exponentials(6)
+        exponentials(7)
+        for t in (2, 3):
+            normalise(t)
+        transpose_attention(2, 2)
+        quantise_attention(0, 2)
+        multiply(0)
+        multiply(1)
+        group_attention(2, 2)
+        reciprocals_of_sums(4, 2)
+        store(0, acopy)
+
+        for t in (4, 5):
+            normalise(t)
+        transpose_attention(4, 2)
+        store(1, acopy)
+        quantise_attention(2, 2)
+        multiply(2)
+        multiply(3)
+        reciprocals_of_sums(6, 2)
+        quantise(v_grouped[1], v_codes[1], v_scales[1])
+        group_attention(4, 2)
+        for t in (6, 7):
+            normalise(t)
+        transpose_attention(6, 2)
+        store(2, acopy)
+        quantise_attention(4, 2)
+        multiply(4)
+        multiply(5)
+        store(3, vcopy)
+        group_attention(6, 2)
+        store(4, acopy)
+        quantise_attention(6, 2)
+        multiply(6)
+        multiply(7, 2)
+        store(5, vcopy)
+        store(6, acopy)
+        store(7, vcopy, 0, 2)
+        store(7, acopy, 1, 2)

@@ -22,7 +22,6 @@ N_TILES = B * ROW_TILES
 LOG2E = 1.0 / math.log(2.0)
 EPS = 1e-8
 TINY = 2.0**-116
-HUGE = 2.0**117
 ROOT_HALF = math.sqrt(0.5)
 FLOPS = B * 2 * (2 * LQ * LK * D)
 
@@ -197,6 +196,7 @@ def tile_adaptiveattention_pb_kernel(tc, q_tanh, k_tanh, value, scoring_weights,
             copy(out=row_sb[:], in_=row[:])
 
         dot = {}
+        partial = {}
         cos_factor = {}
 
         def dot_product(t):
@@ -212,16 +212,19 @@ def tile_adaptiveattention_pb_kernel(tc, q_tanh, k_tanh, value, scoring_weights,
                 stop=True,
             )
 
-        def half_squared_distance(t):
-            b, r = divmod(t, ROW_TILES)
+        def partial_distance(t):
+            partial[t] = batch.tile([P, LK], F32, name="partial")
             nc.vector.scalar_tensor_tensor(
-                out=dist[:, t, :], in0=half_kn2_row[b][:], scalar=half_norm2[b][:, ROW_TILES + r : ROW_TILES + r + 1],
-                in1=dot[t][:], op0=ALU.add, op1=ALU.subtract,
+                out=partial[t][:], in0=dot[t][:], scalar=-1.0, in1=half_kn2_row[t // ROW_TILES][:],
+                op0=ALU.mult, op1=ALU.add,
             )
 
-        def clamp(first, n):
-            tiles = dist[:, first : first + n, :]
-            nc.vector.tensor_scalar(out=tiles, in0=tiles, scalar1=0.0, scalar2=HUGE, op0=ALU.max, op1=ALU.min)
+        def half_squared_distance(t):
+            b, r = divmod(t, ROW_TILES)
+            nc.vector.tensor_scalar(
+                out=dist[:, t, :], in0=partial[t][:], scalar1=half_norm2[b][:, ROW_TILES + r : ROW_TILES + r + 1],
+                scalar2=0.0, op0=ALU.add, op1=ALU.max,
+            )
 
         def square_roots(first, n):
             tiles = dist[:, first : first + n, :]
@@ -374,13 +377,14 @@ def tile_adaptiveattention_pb_kernel(tc, q_tanh, k_tanh, value, scoring_weights,
         group_features(k1, 0, k_grouped[1], vcopy)
         group_features(k1, 1, k_grouped[1], acopy)
         norms(0)
-        half_squared_distance(0)
-        half_squared_distance(1)
+        partial_distance(0)
+        partial_distance(1)
         inverse_norms(0)
         scale_inverse_norms(0)
-        half_squared_distance(2)
-        clamp(0, 2)
-        half_squared_distance(3)
+        partial_distance(2)
+        half_squared_distance(0)
+        half_squared_distance(1)
+        partial_distance(3)
         for r in range(3):
             square(k_sb[1], 1, K, r)
         spread(inv_norm[0], inv_kn_row[0], acopy)
@@ -392,7 +396,8 @@ def tile_adaptiveattention_pb_kernel(tc, q_tanh, k_tanh, value, scoring_weights,
         for r in range(ROW_TILES - 0, ROW_TILES):
             squares_on_tensor(k_grouped[1], 1, K, r)
         quantise(k_grouped[1], k_codes[1], k_scales[1])
-        clamp(2, 2)
+        half_squared_distance(2)
+        half_squared_distance(3)
         group_features(q1, 0, q_grouped[1], acopy)
         group_features(q1, 1, q_grouped[1], vcopy)
         square(q_sb[1], 1, Q, 0)
@@ -413,16 +418,18 @@ def tile_adaptiveattention_pb_kernel(tc, q_tanh, k_tanh, value, scoring_weights,
             regroup_values(1, c)
         for t in range(4, 8):
             dot_product(t)
-        half_squared_distance(4)
+        partial_distance(4)
         inverse_norms(1)
         scale_inverse_norms(1)
         spread(inv_norm[1], inv_kn_row[1], acopy)
+        partial_distance(5)
+        partial_distance(6)
+        half_squared_distance(4)
         half_squared_distance(5)
+        partial_distance(7)
         half_squared_distance(6)
-        clamp(4, 2)
-        half_squared_distance(7)
         final_scores(0, 1)
-        clamp(6, 2)
+        half_squared_distance(7)
         final_scores(1, 1)
         square_roots(4, 2)
 

@@ -271,9 +271,9 @@ def tile_adaptiveattention_pb_kernel(tc, q_tanh, k_tanh, value, scoring_weights,
         a_scales = {}
         product = {}
 
-        def final_scores(first, n):
+        def final_scores(first, n, engine=nc.vector):
             tiles = slice(first, first + n)
-            nc.vector.tensor_tensor(
+            engine.tensor_tensor(
                 out=scores[:, tiles, :], in0=dot_cos[:, tiles, :], in1=dist[:, tiles, :], op=ALU.subtract
             )
 
@@ -399,7 +399,7 @@ def tile_adaptiveattention_pb_kernel(tc, q_tanh, k_tanh, value, scoring_weights,
         half_squared_distance(2)
         half_squared_distance(3)
         group_features(q1, 0, q_grouped[1], acopy)
-        group_features(q1, 1, q_grouped[1], vcopy)
+        group_features(q1, 1, q_grouped[1], acopy)
         square(q_sb[1], 1, Q, 0)
         spread(half_norm2[1], half_kn2_row[1], acopy)
         for r in range(1, ROW_TILES - 0):
@@ -413,7 +413,6 @@ def tile_adaptiveattention_pb_kernel(tc, q_tanh, k_tanh, value, scoring_weights,
         dot_and_cosine(3)
         norms(1)
         square_roots(0, 2)
-        square_roots(2, 2)
         for c in range(PIECES):
             regroup_values(1, c)
         for t in range(4, 8):
@@ -432,7 +431,7 @@ def tile_adaptiveattention_pb_kernel(tc, q_tanh, k_tanh, value, scoring_weights,
         half_squared_distance(7)
         final_scores(1, 1)
         square_roots(4, 2)
-
+        square_roots(2, 2)
         square_roots(6, 2)
         for t in (4, 5):
             cosine_factor(t)
@@ -440,7 +439,8 @@ def tile_adaptiveattention_pb_kernel(tc, q_tanh, k_tanh, value, scoring_weights,
         exponentials(0)
         exponentials(1)
         cosine_factor(6)
-        final_scores(2, 2)
+        final_scores(2, 1, nc.gpsimd)
+        final_scores(3, 1, nc.gpsimd)
         dot_and_cosine(4)
         dot_and_cosine(5)
         row_maxima(2, 2)

@@ -79,19 +79,21 @@ def tile_adaptiveattention_pb_kernel(tc, q_tanh, k_tanh, value, scoring_weights,
 
         for b in range(B):
             k_rows = k_tanh[b].rearrange("(r p) d -> p r d", p=P)
-            pieces = 2 if b == 0 else 1
+            pieces = ROW_TILES if b == 0 else 1
             tiles = ROW_TILES // pieces
             for i in range(pieces):
                 nc.sync.dma_start(
                     out=k_sb[b][:, i * tiles : (i + 1) * tiles, :], in_=k_rows[:, i * tiles : (i + 1) * tiles, :]
                 )
             q_rows = q_tanh[b].rearrange("(p r) d -> p r d", r=ROW_TILES)
+            pieces = 2 if b == 0 else 1
+            tiles = ROW_TILES // pieces
             for i in range(pieces):
                 nc.sync.dma_start(
                     out=q_sb[b][:, i * tiles : (i + 1) * tiles, :], in_=q_rows[:, i * tiles : (i + 1) * tiles, :]
                 )
-            if b == 0:
-                nc.sync.dma_start(out=w_raw[0:1, 0:3], in_=scoring_weights.unsqueeze(0))
+        nc.sync.dma_start(out=w_raw[0:1, 0:3], in_=scoring_weights.unsqueeze(0))
+        for b in range(B):
             nc.sync.dma_start(
                 out=v_sb[b][:].rearrange("p (u e) d -> p u (e d)", u=HALVES),
                 in_=value[b].rearrange("(u p e) d -> p u (e d)", u=HALVES, p=P),
@@ -360,21 +362,19 @@ def tile_adaptiveattention_pb_kernel(tc, q_tanh, k_tanh, value, scoring_weights,
         for pair in range(2):
             group_features(k0, pair, k_grouped[0], vcopy)
         quantise(k_grouped[0], k_codes[0], k_scales[0])
-        for c in range(PIECES):
-            regroup_values(0, c)
         for pair in range(2):
             group_features(q0, pair, q_grouped[0], vcopy)
         for r in range(2):
             square(q_sb[0], 0, Q, r)
         spread(half_norm2[0], half_kn2_row[0], acopy)
         quantise(q_grouped[0], q_codes[0], q_scales[0])
-        mixing_weights()
         for r in range(2, ROW_TILES):
             square(q_sb[0], 0, Q, r)
         k1 = transpose_features(k_sb[1])
+        group_features(k1, 0, k_grouped[1], vcopy)
+        mixing_weights()
         for t in range(4):
             dot_product(t)
-        group_features(k1, 0, k_grouped[1], vcopy)
         group_features(k1, 1, k_grouped[1], acopy)
         norms(0)
         partial_distance(0)
@@ -414,6 +414,8 @@ def tile_adaptiveattention_pb_kernel(tc, q_tanh, k_tanh, value, scoring_weights,
         norms(1)
         square_roots(0, 2)
         for c in range(PIECES):
+            regroup_values(0, c)
+        for c in range(2):
             regroup_values(1, c)
         for t in range(4, 8):
             dot_product(t)
@@ -441,6 +443,8 @@ def tile_adaptiveattention_pb_kernel(tc, q_tanh, k_tanh, value, scoring_weights,
         cosine_factor(6)
         final_scores(2, 1, nc.gpsimd)
         final_scores(3, 1, nc.gpsimd)
+        for c in range(2, PIECES):
+            regroup_values(1, c)
         dot_and_cosine(4)
         dot_and_cosine(5)
         row_maxima(2, 2)

import math
from contextlib import ExitStack

import concourse.mybir as mybir
from concourse.masks import make_identity

F32 = mybir.dt.float32
BF16 = mybir.dt.bfloat16
U32 = mybir.dt.uint32
U8 = mybir.dt.uint8
FP8X4 = mybir.dt.float8_e4m3fn_x4
ACT = mybir.ActivationFunctionType
ALU = mybir.AluOpType
AXIS = mybir.AxisListType

B, LQ, LK, D = 2, 512, 512, 512
P = 128
PACK = 4
HALVES = 2
ROW_TILES = LQ // P
N_TILES = B * ROW_TILES
LOG2E = 1.0 / math.log(2.0)
EPS = 1e-8
TINY = 2.0**-116
ROOT_HALF = math.sqrt(0.5)
FLOPS = B * 2 * (2 * LQ * LK * D)


def tile_adaptiveattention_pb_kernel(tc, q_tanh, k_tanh, value, scoring_weights, out):
    nc = tc.nc
    with ExitStack() as ctx:
        keep = ctx.enter_context(tc.tile_pool(name="keep", bufs=1))
        batch = ctx.enter_context(tc.tile_pool(name="batch", bufs=ROW_TILES))
        work = ctx.enter_context(tc.tile_pool(name="work", bufs=N_TILES))
        results = ctx.enter_context(tc.tile_pool(name="results", bufs=N_TILES))
        psum_t = ctx.enter_context(tc.psum_pool(name="psum_t", bufs=4))
        psum_mx = ctx.enter_context(tc.psum_pool(name="psum_mx", bufs=4))
        ctx.enter_context(tc.manual_schedule())

        ident = keep.tile([P, P], F32)
        ones = keep.tile([P, P], BF16)
        k_sb = [keep.tile([P, ROW_TILES, D], BF16, name="k_sb%d" % b) for b in range(B)]
        q_sb = [keep.tile([P, ROW_TILES, D], BF16, name="q_sb%d" % b) for b in range(B)]
        v_sb = [keep.tile([P, PACK, D], BF16, name="v_sb%d" % b) for b in range(B)]
        k_grouped = [keep.tile([P, LK, PACK], BF16, name="k_grouped%d" % b, align_bytes=64) for b in range(B)]
        q_grouped = [keep.tile([P, LQ, PACK], BF16, name="q_grouped%d" % b, align_bytes=64) for b in range(B)]
        v_grouped = [keep.tile([P, D, PACK], BF16, name="v_grouped%d" % b, align_bytes=64) for b in range(B)]
        k_codes = [keep.tile([P, LK], U32, name="k_codes%d" % b, align_bytes=64) for b in range(B)]
        q_codes = [keep.tile([P, LQ], U32, name="q_codes%d" % b, align_bytes=64) for b in range(B)]
        v_codes = [keep.tile([P, D], U32, name="v_codes%d" % b, align_bytes=64) for b in range(B)]
        k_scales = [keep.tile([P, LK], U8, name="k_scales%d" % b, align_bytes=64) for b in range(B)]
        q_scales = [keep.tile([P, LQ], U8, name="q_scales%d" % b, align_bytes=64) for b in range(B)]
        v_scales = [keep.tile([P, D], U8, name="v_scales%d" % b, align_bytes=64) for b in range(B)]
        half_norm2 = [keep.tile([P, 2 * ROW_TILES], F32, name="half_norm2_%d" % b) for b in range(B)]
        norm = [keep.tile([P, 2 * ROW_TILES], F32, name="norm_%d" % b) for b in range(B)]
        inv_norm = [keep.tile([P, 2 * ROW_TILES], F32, name="inv_norm%d" % b) for b in range(B)]
        w1_inv_qn = [keep.tile([P, ROW_TILES], F32, name="w1_inv_qn%d" % b) for b in range(B)]
        half_kn2_row = [keep.tile([P, LK], F32, name="half_kn2_row%d" % b) for b in range(B)]
        inv_kn_row = [keep.tile([P, LK], F32, name="inv_kn_row%d" % b) for b in range(B)]
        dot_cos = keep.tile([P, N_TILES, LK], F32)
        dist = keep.tile([P, N_TILES, LK], F32)
        scores = keep.tile([P, N_TILES, LK], F32)
        neg_max = keep.tile([P, N_TILES], F32)
        exp_sum = keep.tile([P, N_TILES], F32)
        inv_sum = keep.tile([P, N_TILES], F32)
        tiny = keep.tile([P, 1], F32)
        tiny_root = keep.tile([P, 1], F32)
        w_raw = keep.tile([P, PACK], BF16)
        two = keep.tile([P, 3], F32)
        minus_one = keep.tile([P, 1], F32)

        nc.vector.memset(w_raw[:], 0.0)
        nc.vector.memset(tiny[:], TINY)
        nc.scalar.activation(out=tiny_root[:], in_=tiny[:], func=ACT.Sqrt)
        make_identity(nc, ident[:])
        nc.gpsimd.memset(ones[:], 1.0)
        nc.gpsimd.memset(two[:], 2.0)
        nc.gpsimd.memset(minus_one[:], -1.0)

        for b in range(B):
            k_rows = k_tanh[b].rearrange("(r p) d -> p r d", p=P)
            pieces = ROW_TILES if b == 0 else 1
            tiles = ROW_TILES // pieces
            for i in range(pieces):
                nc.sync.dma_start(
                    out=k_sb[b][:, i * tiles : (i + 1) * tiles, :], in_=k_rows[:, i * tiles : (i + 1) * tiles, :]
                )
            q_rows = q_tanh[b].rearrange("(p r) d -> p r d", r=ROW_TILES)
            pieces = 2 if b == 0 else 1
            tiles = ROW_TILES // pieces
            for i in range(pieces):
                nc.sync.dma_start(
                    out=q_sb[b][:, i * tiles : (i + 1) * tiles, :], in_=q_rows[:, i * tiles : (i + 1) * tiles, :]
                )
        nc.sync.dma_start(out=w_raw[0:1, 0:3], in_=scoring_weights.unsqueeze(0))
        for b in range(B):
            nc.sync.dma_start(
                out=v_sb[b][:].rearrange("p (u e) d -> p u (e d)", u=HALVES),
                in_=value[b].rearrange("(u p e) d -> p u (e d)", u=HALVES, p=P),
            )

        w_neg_max = keep.tile([P, 1], F32)
        w_log2 = keep.tile([P, 3], F32)
        w_exp = keep.tile([P, 3], F32)
        w_sum = keep.tile([P, 1], F32)
        w_inv_sum = keep.tile([P, 1], F32)
        w = keep.tile([P, 3], F32)
        cos_cap = keep.tile([P, 1], F32)
        twice_w2_squared = keep.tile([P, 1], F32)

        def mixing_weights():
            w_all = psum_t.tile([P, 3], F32, tag="t", name="w_all")
            nc.tensor.matmul(w_all[:], lhsT=ones[:], rhs=w_raw[:, 0:3], start=True, stop=True)
            nc.vector.tensor_reduce(out=w_neg_max[:], in_=w_all[:], axis=AXIS.X, op=ALU.max, negate=True)
            nc.vector.tensor_scalar(
                out=w_log2[:], in0=w_all[:], scalar1=w_neg_max[:], scalar2=LOG2E, op0=ALU.add, op1=ALU.mult
            )
            nc.gpsimd.tensor_tensor(out=w_exp[:], in0=two[:], in1=w_log2[:], op=ALU.pow)
            nc.gpsimd.tensor_scalar(
                out=w_sum[:], in0=w_exp[:, 0:1], scalar1=w_exp[:, 1:2], scalar2=w_exp[:, 2:3], op0=ALU.add, op1=ALU.add
            )
            nc.gpsimd.tensor_tensor(out=w_inv_sum[:], in0=w_sum[:], in1=minus_one[:], op=ALU.pow)
            nc.gpsimd.tensor_scalar(out=w[:], in0=w_exp[:], scalar1=w_inv_sum[:], scalar2=0.0, op0=ALU.mult, op1=ALU.add)
            nc.gpsimd.tensor_scalar(
                out=cos_cap[:], in0=w[:, 1:2], scalar1=1.0 / EPS, scalar2=w[:, 0:1], op0=ALU.mult, op1=ALU.add
            )
            nc.gpsimd.tensor_scalar(
                out=twice_w2_squared[:], in0=w[:, 2:3], scalar1=w[:, 2:3], scalar2=2.0, op0=ALU.mult, op1=ALU.mult
            )

        def transpose_features(x_sb):
            x_words = x_sb[:].bitcast(F32)
            banks = {}
            for pair in range(ROW_TILES // 2):
                xt = psum_t.tile([P, HALVES, 2 * P], F32, tag="t", name="xt")
                for i in range(2):
                    for u in range(HALVES):
                        nc.tensor.transpose(
                            xt[:, u, i * P : (i + 1) * P],
                            x_words[:, 2 * pair + i, u * P : (u + 1) * P],
                            ident[:],
                        )
                banks[pair] = xt
            return banks

        def group_features(banks, pair, x_grouped, copy):
            grouped_words = x_grouped[:].bitcast(F32)
            copy(
                out=grouped_words[:, 2 * pair * P : 2 * (pair + 1) * P, :],
                in_=banks[pair][:].rearrange("p u c -> p c u"),
            )

        def square(x_sb, b, first, r):
            squares = work.tile([P, D], BF16, name="squares")
            nc.scalar.activation(
                out=squares[:], in_=x_sb[:, r, :], func=ACT.Square, scale=ROOT_HALF,
                accum_out=half_norm2[b][:, first + r : first + r + 1],
            )

        def squares_on_tensor(x_grouped, b, first, r):
            gram = psum_t.tile([P, P], F32, tag="t", name="gram")
            rows = slice(r * P, (r + 1) * P)
            for j in range(PACK):
                nc.tensor.matmul(
                    gram[:], lhsT=x_grouped[:, rows, j], rhs=x_grouped[:, rows, j], start=(j == 0), stop=(j == PACK - 1)
                )
            diagonal = work.tile([P, P], F32, name="diagonal")
            nc.vector.scalar_tensor_tensor(
                out=diagonal[:], in0=gram[:], scalar=0.5, in1=ident[:], op0=ALU.mult, op1=ALU.mult,
                accum_out=half_norm2[b][:, first + r : first + r + 1],
            )

        def norms(b):
            nc.scalar.activation(out=norm[b][:], in_=half_norm2[b][:], func=ACT.Sqrt, scale=2.0, bias=tiny[:])

        def inverse_norms(b):
            nc.vector.reciprocal(out=inv_norm[b][:], in_=norm[b][:])

        def scale_inverse_norms(b):
            nc.gpsimd.tensor_scalar(
                out=w1_inv_qn[b][:], in0=inv_norm[b][:, ROW_TILES:], scalar1=w[:, 1:2], scalar2=0.0,
                op0=ALU.mult, op1=ALU.add,
            )

        def quantise(x_grouped, x_codes, x_scales):
            nc.vector.quantize_mx(
                out=x_codes[:].bitcast(FP8X4),
                scales=x_scales[:],
                in_=x_grouped[:].rearrange("p c t -> p (c t)"),
            )

        def spread(columns, row_sb, copy):
            row = psum_t.tile([P, LK], F32, tag="t")
            for r in range(ROW_TILES):
                nc.tensor.transpose(
                    row[:, r * P : (r + 1) * P], columns[:, r : r + 1].to_broadcast([P, P]), ident[:]
                )
            copy(out=row_sb[:], in_=row[:])

        dot = {}
        partial = {}
        cos_factor = {}

        def dot_product(t):
            b, r = divmod(t, ROW_TILES)
            dot[t] = psum_mx.tile([P, LK], F32, tag="mx", name="dot")
            nc.tensor.matmul_mx(
                out=dot[t][:],
                lhsT=q_codes[b][:, r * P : (r + 1) * P].bitcast(FP8X4),
                lhsT_scale=q_scales[b][:, r * P : (r + 1) * P],
                rhs=k_codes[b][:].bitcast(FP8X4),
                rhs_scale=k_scales[b][:],
                start=True,
                stop=True,
            )

        def partial_distance(t):
            partial[t] = batch.tile([P, LK], F32, name="partial")
            nc.vector.scalar_tensor_tensor(
                out=partial[t][:], in0=dot[t][:], scalar=-1.0, in1=half_kn2_row[t // ROW_TILES][:],
                op0=ALU.mult, op1=ALU.add,
            )

        def half_squared_distance(t):
            b, r = divmod(t, ROW_TILES)
            nc.vector.tensor_scalar(
                out=dist[:, t, :], in0=partial[t][:], scalar1=half_norm2[b][:, ROW_TILES + r : ROW_TILES + r + 1],
                scalar2=0.0, op0=ALU.add, op1=ALU.max,
            )

        def square_roots(first, n):
            tiles = dist[:, first : first + n, :]
            nc.scalar.activation(out=tiles, in_=tiles, func=ACT.Sqrt, scale=twice_w2_squared[:], bias=tiny[:])

        def cosine_factor(t):
            b, r = divmod(t, ROW_TILES)
            cos_factor[t] = batch.tile([P, LK], F32, name="cos_factor")
            if t in COS_ON_VECTOR:
                nc.vector.tensor_scalar(
                    out=cos_factor[t][:], in0=inv_kn_row[b][:], scalar1=w1_inv_qn[b][:, r : r + 1], scalar2=w[:, 0:1],
                    op0=ALU.mult, op1=ALU.add,
                )
                return
            if t in COS_ON_SCALAR:
                nc.scalar.activation(
                    out=cos_factor[t][:], in_=inv_kn_row[b][:], func=ACT.Identity,
                    scale=w1_inv_qn[b][:, r : r + 1], bias=w[:, 0:1],
                )
                return
            nc.gpsimd.tensor_scalar(
                out=cos_factor[t][:], in0=inv_kn_row[b][:], scalar1=w1_inv_qn[b][:, r : r + 1], scalar2=w[:, 0:1],
                op0=ALU.mult, op1=ALU.add,
            )

        def dot_and_cosine(t):
            nc.vector.scalar_tensor_tensor(
                out=dot_cos[:, t, :], in0=cos_factor[t][:], scalar=cos_cap[:], in1=dot[t][:], op0=ALU.min, op1=ALU.mult
            )

        def regroup_values(b, c):
            width = D // PIECES
            cols = slice(c * width, (c + 1) * width)
            nc.gpsimd.tensor_scalar(
                out=v_grouped[b][:, cols, :], in0=v_sb[b][:, :, cols].rearrange("p t d -> p d t"),
                scalar1=1.0, scalar2=0.0, op0=ALU.mult, op1=ALU.add,
            )

        prob = {}
        attn = {}
        attn_t = {}
        a_grouped = {}
        a_codes = {}
        a_scales = {}
        product = {}

        def final_scores(first, n, engine=nc.vector):
            tiles = slice(first, first + n)
            engine.tensor_tensor(
                out=scores[:, tiles, :], in0=dot_cos[:, tiles, :], in1=dist[:, tiles, :], op=ALU.subtract
            )

        def row_maxima(first, n):
            tiles = slice(first, first + n)
            nc.vector.tensor_reduce(
                out=neg_max[:, tiles], in_=scores[:, tiles, :], axis=AXIS.X, op=ALU.max, negate=True
            )

        def exponentials(t):
            prob[t] = work.tile([P, LK], F32, name="prob")
            nc.scalar.activation(
                out=prob[t][:], in_=scores[:, t, :], func=ACT.Exp, bias=neg_max[:, t : t + 1],
                accum_out=exp_sum[:, t : t + 1],
            )

        def reciprocals_of_sums(first, n):
            tiles = slice(first, first + n)
            nc.vector.reciprocal(out=inv_sum[:, tiles], in_=exp_sum[:, tiles])

        def normalise(t):
            attn[t] = work.tile([P, LK], BF16, name="attn")
            if t in ON_SCALAR:
                nc.scalar.activation(out=attn[t][:], in_=prob[t][:], func=ACT.Copy, scale=inv_sum[:, t : t + 1])
                return
            nc.vector.tensor_scalar(
                out=attn[t][:], in0=prob[t][:], scalar1=inv_sum[:, t : t + 1], scalar2=None, op0=ALU.mult
            )

        def transpose_attention(first, n):
            attn_t[first] = psum_t.tile([P, n, HALVES, P], F32, tag="t", name="attn_t")
            for i in range(n):
                attn_words = attn[first + i][:].bitcast(F32)
                for u in range(HALVES):
                    nc.tensor.transpose(attn_t[first][:, i, u, :], attn_words[:, u * P : (u + 1) * P], ident[:])

        def group_attention(first, n):
            a_grouped[first] = work.tile([P, n * P, PACK], BF16, name="a_grouped%d" % n, align_bytes=64)
            nc.scalar.copy(
                out=a_grouped[first][:].bitcast(F32).rearrange("p (t i) u -> p t i u", t=n),
                in_=attn_t[first][:].rearrange("p t u i -> p t i u"),
            )

        def quantise_attention(first, n):
            codes = work.tile([P, n * P], U32, name="a_codes%d" % n, align_bytes=64)
            scales = work.tile([P, n * P], U8, name="a_scales%d" % n, align_bytes=64)
            quantise(a_grouped[first], codes, scales)
            for i in range(n):
                a_codes[first + i] = codes[:, i * P : (i + 1) * P]
                a_scales[first + i] = scales[:, i * P : (i + 1) * P]

        def multiply(t, parts=1):
            b = t // ROW_TILES
            for i in range(parts):
                cols = slice(i * D // parts, (i + 1) * D // parts)
                product[t, i] = psum_mx.tile([P, D // parts], F32, tag="mx", name="product")
                nc.tensor.matmul_mx(
                    out=product[t, i][:],
                    lhsT=a_codes[t].bitcast(FP8X4),
                    lhsT_scale=a_scales[t],
                    rhs=v_codes[b][:, cols].bitcast(FP8X4),
                    rhs_scale=v_scales[b][:, cols],
                    start=True,
                    stop=True,
                )

        def store(t, copy, part=0, parts=1):
            b, r = divmod(t, ROW_TILES)
            cols = slice(part * D // parts, (part + 1) * D // parts)
            result = results.tile([P, D // parts], F32, name="result")
            copy(out=result[:], in_=product[t, part][:])
            nc.sync.dma_start(out=out[b].rearrange("(p r) d -> p r d", r=ROW_TILES)[:, r, cols], in_=result[:])

        vcopy, acopy = nc.vector.tensor_copy, nc.scalar.copy
        K, Q = 0, ROW_TILES
        PIECES = 4
        ON_SCALAR = (0, 1)
        COS_ON_SCALAR = (4, 5, 6, 7)
        COS_ON_VECTOR = ()
        k0 = transpose_features(k_sb[0])
        q0 = transpose_features(q_sb[0])
        for r in range(ROW_TILES):
            square(k_sb[0], 0, K, r)
        for pair in range(2):
            group_features(k0, pair, k_grouped[0], vcopy)
        quantise(k_grouped[0], k_codes[0], k_scales[0])
        for pair in range(2):
            group_features(q0, pair, q_grouped[0], vcopy)
        for r in range(2):
            square(q_sb[0], 0, Q, r)
        spread(half_norm2[0], half_kn2_row[0], acopy)
        quantise(q_grouped[0], q_codes[0], q_scales[0])
        for r in range(2, ROW_TILES):
            square(q_sb[0], 0, Q, r)
        k1 = transpose_features(k_sb[1])
        group_features(k1, 0, k_grouped[1], vcopy)
        mixing_weights()
        for t in range(4):
            dot_product(t)
        group_features(k1, 1, k_grouped[1], acopy)
        norms(0)
        partial_distance(0)
        partial_distance(1)
        inverse_norms(0)
        scale_inverse_norms(0)
        partial_distance(2)
        half_squared_distance(0)
        half_squared_distance(1)
        partial_distance(3)
        for r in range(3):
            square(k_sb[1], 1, K, r)
        spread(inv_norm[0], inv_kn_row[0], acopy)
        for t in range(4):
            cosine_factor(t)
        q1 = transpose_features(q_sb[1])
        for r in range(3, ROW_TILES - 0):
            square(k_sb[1], 1, K, r)
        for r in range(ROW_TILES - 0, ROW_TILES):
            squares_on_tensor(k_grouped[1], 1, K, r)
        quantise(k_grouped[1], k_codes[1], k_scales[1])
        half_squared_distance(2)
        half_squared_distance(3)
        group_features(q1, 0, q_grouped[1], acopy)
        group_features(q1, 1, q_grouped[1], acopy)
        square(q_sb[1], 1, Q, 0)
        spread(half_norm2[1], half_kn2_row[1], acopy)
        for r in range(1, ROW_TILES - 0):
            square(q_sb[1], 1, Q, r)
        dot_and_cosine(0)
        quantise(q_grouped[1], q_codes[1], q_scales[1])
        for t in range(1, 3):
            dot_and_cosine(t)
        for r in range(ROW_TILES - 0, ROW_TILES):
            squares_on_tensor(q_grouped[1], 1, Q, r)
        dot_and_cosine(3)
        norms(1)
        square_roots(0, 2)
        for c in range(PIECES):
            regroup_values(0, c)
        for c in range(2):
            regroup_values(1, c)
        for t in range(4, 8):
            dot_product(t)
        partial_distance(4)
        inverse_norms(1)
        scale_inverse_norms(1)
        spread(inv_norm[1], inv_kn_row[1], acopy)
        partial_distance(5)
        partial_distance(6)
        half_squared_distance(4)
        half_squared_distance(5)
        partial_distance(7)
        half_squared_distance(6)
        final_scores(0, 1)
        half_squared_distance(7)
        final_scores(1, 1)
        square_roots(4, 2)
        square_roots(2, 2)
        square_roots(6, 2)
        for t in (4, 5):
            cosine_factor(t)
        row_maxima(0, 2)
        exponentials(0)
        exponentials(1)
        cosine_factor(6)
        final_scores(2, 1, nc.gpsimd)
        final_scores(3, 1, nc.gpsimd)
        for c in range(2, PIECES):
            regroup_values(1, c)
        dot_and_cosine(4)
        dot_and_cosine(5)
        row_maxima(2, 2)
        exponentials(2)
        cosine_factor(7)
        exponentials(3)
        quantise(v_grouped[0], v_codes[0], v_scales[0])
        final_scores(4, 2)
        reciprocals_of_sums(0, 2)
        dot_and_cosine(6)
        row_maxima(4, 2)
        for t in (0, 1):
            normalise(t)
        transpose_attention(0, 2)
        exponentials(4)
        exponentials(5)
        group_attention(0, 2)
        dot_and_cosine(7)
        final_scores(6, 2)
        reciprocals_of_sums(2, 2)
        row_maxima(6, 2)
        exponentials(6)
        exponentials(7)
        for t in (2, 3):
            normalise(t)
        transpose_attention(2, 2)
        quantise_attention(0, 2)
        multiply(0)
        multiply(1)
        group_attention(2, 2)
        reciprocals_of_sums(4, 2)
        store(0, acopy)

        for t in (4, 5):
            normalise(t)
        transpose_attention(4, 2)
        store(1, acopy)
        quantise_attention(2, 2)
        multiply(2)
        multiply(3)
        reciprocals_of_sums(6, 2)
        quantise(v_grouped[1], v_codes[1], v_scales[1])
        group_attention(4, 2)
        for t in (6, 7):
            normalise(t)
        transpose_attention(6, 2)
        store(2, acopy)
        quantise_attention(4, 2)
        multiply(4)
        multiply(5)
        store(3, vcopy)
        group_attention(6, 2)
        store(4, acopy)
        quantise_attention(6, 2)
        multiply(6)
        multiply(7, 2)
        store(5, vcopy)
        store(6, acopy)
        store(7, vcopy, 0, 2)
        store(7, acopy, 1, 2)
